import numpy as np
import ml_dtypes

BF16 = ml_dtypes.bfloat16


def bf(x):
    return np.asarray(x, np.float32).astype(BF16)


def f32(x):
    return np.asarray(x, np.float32)


def f64(x):
    return np.asarray(x).astype(np.float64)


def striped(idx):
    return np.tile(idx.reshape(-1, 16).T, (8, 1))


C, S, K, H, R, N = 512, 2048, 4, 1024, 8, 8192
ALPHA = 0.2


def setup_inputs():
    return {"x": f32(np.random.standard_normal((C, S))), "w": bf(np.random.standard_normal((C + C, C)) / np.sqrt(C)), "offs": striped(np.concatenate([np.random.permutation(S)[:H] for _ in range(R)]))}


def reference(x, w, offs):
    idx = offs[:16].T.reshape(-1)
    xs = f64(x)
    neigh = xs[:, idx].reshape(C, K, S).sum(axis=1) / K
    v = f64(w)[:C].T @ xs + f64(w)[C:].T @ neigh
    return np.maximum(v, ALPHA * v)

@@ -1,0 +1,77 @@
+import concourse.mybir as mybir
+
+F32, BF16, U16 = mybir.dt.float32, mybir.dt.bfloat16, mybir.dt.uint16
+ADD = mybir.AluOpType.add
+COPY, RELU = mybir.ActivationFunctionType.Copy, mybir.ActivationFunctionType.Relu
+
+P = 128
+FEATURES = 512
+NODES = 2048
+NEIGHBOURS = 4
+SLOPE = 0.2
+BLOCKS = FEATURES // P
+CHUNK = 512
+CHUNKS = NODES // CHUNK
+PER_COLUMN = 16
+
+FLOPS = 2 * (2 * FEATURES) * FEATURES * NODES
+
+
+def tile_dyngraphsage_kernel(tc, x, w, offs, out):
+    nc = tc.nc
+    with (
+        tc.tile_pool(name="held", bufs=1) as held,
+        tc.tile_pool(name="sums", bufs=2 * NEIGHBOURS) as sums,
+        tc.tile_pool(name="means", bufs=2 * BLOCKS) as means,
+        tc.tile_pool(name="staged", bufs=4) as staged,
+        tc.psum_pool(name="psum", bufs=2) as psum,
+    ):
+        offsets = held.tile([P, NEIGHBOURS * NODES // PER_COLUMN], U16, name="offsets")
+        nc.sync.dma_start(offsets[:], offs)
+        x_f32 = [held.tile([P, NODES], F32, name=f"x_f32_{c}") for c in range(BLOCKS)]
+        for c in range(BLOCKS):
+            nc.sync.dma_start(x_f32[c][:], x[c * P : (c + 1) * P, :])
+        w_sb = held.tile([P, 2 * BLOCKS, FEATURES], BF16, name="w_sb")
+        nc.sync.dma_start(w_sb[:], w.rearrange("(r p) e -> p r e", p=P))
+
+        zeros = held.tile([P, CHUNK], F32, name="zeros")
+        nc.vector.memset(zeros[:], 0.0)
+
+        x_bf = [held.tile([P, NODES], BF16, name=f"x_bf_{c}") for c in range(BLOCKS)]
+        for c in range(BLOCKS):
+            nc.scalar.activation(x_bf[c][:], x_f32[c][:], COPY)
+
+        for j in range(CHUNKS):
+            nodes = slice(j * CHUNK, (j + 1) * CHUNK)
+
+            v = [psum.tile([P, CHUNK], F32, name=f"v{e}") for e in range(BLOCKS)]
+            for e in range(BLOCKS):
+                for c in range(BLOCKS):
+                    nc.tensor.matmul(
+                        v[e][:], w_sb[:, c, e * P : (e + 1) * P], x_bf[c][:, nodes], start=(c == 0), stop=False
+                    )
+
+            for c in range(BLOCKS):
+                total = zeros
+                for k in range(NEIGHBOURS):
+                    first = (k * NODES + j * CHUNK) // PER_COLUMN
+                    picked = x_f32[c][:].indirect(offsets[:, first : first + CHUNK // PER_COLUMN])
+                    longer = sums.tile([P, CHUNK], F32, name="longer")
+                    nc.vector.tensor_tensor(longer[:], picked, total[:], ADD)
+                    total = longer
+
+                mean = means.tile([P, CHUNK], BF16, name="mean")
+                nc.scalar.activation(mean[:], total[:], COPY, scale=1.0 / NEIGHBOURS)
+                for e in range(BLOCKS):
+                    nc.tensor.matmul(
+                        v[e][:], w_sb[:, BLOCKS + c, e * P : (e + 1) * P], mean[:], start=False, stop=(c == BLOCKS - 1)
+                    )
+
+            for e in range(BLOCKS):
+                sloped = staged.tile([P, CHUNK], F32, name="sloped")
+                nc.scalar.activation(sloped[:], v[e][:], COPY, scale=SLOPE)
+                lifted = staged.tile([P, CHUNK], F32, name="lifted")
+                nc.scalar.activation(lifted[:], v[e][:], RELU, scale=1.0 - SLOPE)
+                result = staged.tile([P, CHUNK], F32, name="result")
+                nc.gpsimd.tensor_tensor(result[:], sloped[:], lifted[:], ADD)
+                nc.sync.dma_start(out[e * P : (e + 1) * P, nodes], result[:])

@@ -21,7 +21,7 @@ def tile_dyngraphsage_kernel(tc, x, w, offs, out):
     nc = tc.nc
     with (
         tc.tile_pool(name="held", bufs=1) as held,
-        tc.tile_pool(name="sums", bufs=2 * NEIGHBOURS) as sums,
+        tc.tile_pool(name="sums", bufs=3 * BLOCKS) as sums,
         tc.tile_pool(name="means", bufs=2 * BLOCKS) as means,
         tc.tile_pool(name="staged", bufs=4) as staged,
         tc.psum_pool(name="psum", bufs=2) as psum,
@@ -51,17 +51,18 @@ def tile_dyngraphsage_kernel(tc, x, w, offs, out):
                         v[e][:], w_sb[:, c, e * P : (e + 1) * P], x_bf[c][:, nodes], start=(c == 0), stop=False
                     )
 
-            for c in range(BLOCKS):
-                total = zeros
-                for k in range(NEIGHBOURS):
-                    first = (k * NODES + j * CHUNK) // PER_COLUMN
+            totals = [zeros] * BLOCKS
+            for k in range(NEIGHBOURS):
+                first = (k * NODES + j * CHUNK) // PER_COLUMN
+                for c in range(BLOCKS):
                     picked = x_f32[c][:].indirect(offsets[:, first : first + CHUNK // PER_COLUMN])
                     longer = sums.tile([P, CHUNK], F32, name="longer")
-                    nc.vector.tensor_tensor(longer[:], picked, total[:], ADD)
-                    total = longer
+                    nc.vector.tensor_tensor(longer[:], picked, totals[c][:], ADD)
+                    totals[c] = longer
 
+            for c in range(BLOCKS):
                 mean = means.tile([P, CHUNK], BF16, name="mean")
-                nc.scalar.activation(mean[:], total[:], COPY, scale=1.0 / NEIGHBOURS)
+                nc.scalar.activation(mean[:], totals[c][:], COPY, scale=1.0 / NEIGHBOURS)
                 for e in range(BLOCKS):
                     nc.tensor.matmul(
                         v[e][:], w_sb[:, BLOCKS + c, e * P : (e + 1) * P], mean[:], start=False, stop=(c == BLOCKS - 1)

@@ -10,9 +10,11 @@ NODES = 2048
 NEIGHBOURS = 4
 SLOPE = 0.2
 BLOCKS = FEATURES // P
-CHUNK = 512
-CHUNKS = NODES // CHUNK
+BANK = 512
 PER_COLUMN = 16
+
+WIDTHS = (BANK, BANK, BANK, BANK // 2, BANK // 4, BANK // 4)
+assert sum(WIDTHS) == NODES
 
 FLOPS = 2 * (2 * FEATURES) * FEATURES * NODES
 
@@ -34,45 +36,48 @@ def tile_dyngraphsage_kernel(tc, x, w, offs, out):
         w_sb = held.tile([P, 2 * BLOCKS, FEATURES], BF16, name="w_sb")
         nc.sync.dma_start(w_sb[:], w.rearrange("(r p) e -> p r e", p=P))
 
-        zeros = held.tile([P, CHUNK], F32, name="zeros")
+        zeros = held.tile([P, BANK], F32, name="zeros")
         nc.vector.memset(zeros[:], 0.0)
 
         x_bf = [held.tile([P, NODES], BF16, name=f"x_bf_{c}") for c in range(BLOCKS)]
         for c in range(BLOCKS):
             nc.scalar.activation(x_bf[c][:], x_f32[c][:], COPY)
 
-        for j in range(CHUNKS):
-            nodes = slice(j * CHUNK, (j + 1) * CHUNK)
+        start = 0
+        for width in WIDTHS:
+            nodes = slice(start, start + width)
 
-            v = [psum.tile([P, CHUNK], F32, name=f"v{e}") for e in range(BLOCKS)]
+            v = [psum.tile([P, width], F32, name=f"v{e}") for e in range(BLOCKS)]
             for e in range(BLOCKS):
                 for c in range(BLOCKS):
                     nc.tensor.matmul(
                         v[e][:], w_sb[:, c, e * P : (e + 1) * P], x_bf[c][:, nodes], start=(c == 0), stop=False
                     )
 
-            totals = [zeros] * BLOCKS
+            totals = [zeros[:, :width]] * BLOCKS
             for k in range(NEIGHBOURS):
-                first = (k * NODES + j * CHUNK) // PER_COLUMN
+                first = (k * NODES + start) // PER_COLUMN
                 for c in range(BLOCKS):
-                    picked = x_f32[c][:].indirect(offsets[:, first : first + CHUNK // PER_COLUMN])
-                    longer = sums.tile([P, CHUNK], F32, name="longer")
-                    nc.vector.tensor_tensor(longer[:], picked, totals[c][:], ADD)
-                    totals[c] = longer
+                    picked = x_f32[c][:].indirect(offsets[:, first : first + width // PER_COLUMN])
+                    longer = sums.tile([P, width], F32, name="longer")
+                    nc.vector.tensor_tensor(longer[:], picked, totals[c], ADD)
+                    totals[c] = longer[:]
 
             for c in range(BLOCKS):
-                mean = means.tile([P, CHUNK], BF16, name="mean")
-                nc.scalar.activation(mean[:], totals[c][:], COPY, scale=1.0 / NEIGHBOURS)
+                mean = means.tile([P, width], BF16, name="mean")
+                nc.scalar.activation(mean[:], totals[c], COPY, scale=1.0 / NEIGHBOURS)
                 for e in range(BLOCKS):
                     nc.tensor.matmul(
                         v[e][:], w_sb[:, BLOCKS + c, e * P : (e + 1) * P], mean[:], start=False, stop=(c == BLOCKS - 1)
                     )
 
             for e in range(BLOCKS):
-                sloped = staged.tile([P, CHUNK], F32, name="sloped")
+                sloped = staged.tile([P, width], F32, name="sloped")
                 nc.scalar.activation(sloped[:], v[e][:], COPY, scale=SLOPE)
-                lifted = staged.tile([P, CHUNK], F32, name="lifted")
+                lifted = staged.tile([P, width], F32, name="lifted")
                 nc.scalar.activation(lifted[:], v[e][:], RELU, scale=1.0 - SLOPE)
-                result = staged.tile([P, CHUNK], F32, name="result")
+                result = staged.tile([P, width], F32, name="result")
                 nc.gpsimd.tensor_tensor(result[:], sloped[:], lifted[:], ADD)
                 nc.sync.dma_start(out[e * P : (e + 1) * P, nodes], result[:])
+
+            start += width

@@ -1,20 +1,19 @@
 import concourse.mybir as mybir
 
 F32, BF16, U16 = mybir.dt.float32, mybir.dt.bfloat16, mybir.dt.uint16
-ADD = mybir.AluOpType.add
+ADD, MAX = mybir.AluOpType.add, mybir.AluOpType.max
 COPY, RELU = mybir.ActivationFunctionType.Copy, mybir.ActivationFunctionType.Relu
 
 P = 128
 FEATURES = 512
 NODES = 2048
 NEIGHBOURS = 4
+WHOLE = 2
 SLOPE = 0.2
 BLOCKS = FEATURES // P
-BANK = 512
+CHUNK = 512
+CHUNKS = NODES // CHUNK
 PER_COLUMN = 16
-
-WIDTHS = (BANK, BANK, BANK, BANK // 2, BANK // 4, BANK // 4)
-assert sum(WIDTHS) == NODES
 
 FLOPS = 2 * (2 * FEATURES) * FEATURES * NODES
 
@@ -23,6 +22,7 @@ def tile_dyngraphsage_kernel(tc, x, w, offs, out):
     nc = tc.nc
     with (
         tc.tile_pool(name="held", bufs=1) as held,
+        tc.tile_pool(name="whole", bufs=2 * BLOCKS) as whole,
         tc.tile_pool(name="sums", bufs=3 * BLOCKS) as sums,
         tc.tile_pool(name="means", bufs=2 * BLOCKS) as means,
         tc.tile_pool(name="staged", bufs=4) as staged,
@@ -36,48 +36,57 @@ def tile_dyngraphsage_kernel(tc, x, w, offs, out):
         w_sb = held.tile([P, 2 * BLOCKS, FEATURES], BF16, name="w_sb")
         nc.sync.dma_start(w_sb[:], w.rearrange("(r p) e -> p r e", p=P))
 
-        zeros = held.tile([P, BANK], F32, name="zeros")
+        zeros = held.tile([P, NODES], F32, name="zeros")
         nc.vector.memset(zeros[:], 0.0)
 
         x_bf = [held.tile([P, NODES], BF16, name=f"x_bf_{c}") for c in range(BLOCKS)]
         for c in range(BLOCKS):
             nc.scalar.activation(x_bf[c][:], x_f32[c][:], COPY)
 
-        start = 0
-        for width in WIDTHS:
-            nodes = slice(start, start + width)
+        totals = [zeros] * BLOCKS
+        for k in range(WHOLE):
+            first = k * NODES // PER_COLUMN
+            for c in range(BLOCKS):
+                picked = x_f32[c][:].indirect(offsets[:, first : first + NODES // PER_COLUMN])
+                longer = whole.tile([P, NODES], F32, name="longer_whole")
+                nc.vector.tensor_tensor(longer[:], picked, totals[c][:], ADD)
+                totals[c] = longer
 
-            v = [psum.tile([P, width], F32, name=f"v{e}") for e in range(BLOCKS)]
+        for j in range(CHUNKS):
+            nodes = slice(j * CHUNK, (j + 1) * CHUNK)
+
+            v = [psum.tile([P, CHUNK], F32, name=f"v{e}") for e in range(BLOCKS)]
             for e in range(BLOCKS):
                 for c in range(BLOCKS):
                     nc.tensor.matmul(
                         v[e][:], w_sb[:, c, e * P : (e + 1) * P], x_bf[c][:, nodes], start=(c == 0), stop=False
                     )
 
-            totals = [zeros[:, :width]] * BLOCKS
-            for k in range(NEIGHBOURS):
-                first = (k * NODES + start) // PER_COLUMN
+            chunk_totals = [totals[c][:, nodes] for c in range(BLOCKS)]
+            for k in range(WHOLE, NEIGHBOURS):
+                first = (k * NODES + j * CHUNK) // PER_COLUMN
                 for c in range(BLOCKS):
-                    picked = x_f32[c][:].indirect(offsets[:, first : first + width // PER_COLUMN])
-                    longer = sums.tile([P, width], F32, name="longer")
-                    nc.vector.tensor_tensor(longer[:], picked, totals[c], ADD)
-                    totals[c] = longer[:]
+                    picked = x_f32[c][:].indirect(offsets[:, first : first + CHUNK // PER_COLUMN])
+                    longer = sums.tile([P, CHUNK], F32, name="longer")
+                    nc.vector.tensor_tensor(longer[:], picked, chunk_totals[c], ADD)
+                    chunk_totals[c] = longer[:]
 
             for c in range(BLOCKS):
-                mean = means.tile([P, width], BF16, name="mean")
-                nc.scalar.activation(mean[:], totals[c], COPY, scale=1.0 / NEIGHBOURS)
+                mean = means.tile([P, CHUNK], BF16, name="mean")
+                nc.scalar.activation(mean[:], chunk_totals[c], COPY, scale=1.0 / NEIGHBOURS)
                 for e in range(BLOCKS):
                     nc.tensor.matmul(
                         v[e][:], w_sb[:, BLOCKS + c, e * P : (e + 1) * P], mean[:], start=False, stop=(c == BLOCKS - 1)
                     )
 
             for e in range(BLOCKS):
-                sloped = staged.tile([P, width], F32, name="sloped")
+                sloped = staged.tile([P, CHUNK], F32, name="sloped")
                 nc.scalar.activation(sloped[:], v[e][:], COPY, scale=SLOPE)
-                lifted = staged.tile([P, width], F32, name="lifted")
-                nc.scalar.activation(lifted[:], v[e][:], RELU, scale=1.0 - SLOPE)
-                result = staged.tile([P, width], F32, name="result")
-                nc.gpsimd.tensor_tensor(result[:], sloped[:], lifted[:], ADD)
+                result = staged.tile([P, CHUNK], F32, name="result")
+                if j < CHUNKS - 1:
+                    lifted = staged.tile([P, CHUNK], F32, name="lifted")
+                    nc.scalar.activation(lifted[:], v[e][:], RELU, scale=1.0 - SLOPE)
+                    nc.gpsimd.tensor_tensor(result[:], sloped[:], lifted[:], ADD)
+                else:
+                    nc.vector.tensor_tensor(result[:], v[e][:], sloped[:], MAX)
                 nc.sync.dma_start(out[e * P : (e + 1) * P, nodes], result[:])
-
-            start += width

@@ -8,11 +8,12 @@ P = 128
 FEATURES = 512
 NODES = 2048
 NEIGHBOURS = 4
-WHOLE = 2
+EARLY = 2
 SLOPE = 0.2
 BLOCKS = FEATURES // P
 CHUNK = 512
-CHUNKS = NODES // CHUNK
+SPAN_CHUNKS = 8 // BLOCKS
+SPAN = SPAN_CHUNKS * CHUNK
 PER_COLUMN = 16
 
 FLOPS = 2 * (2 * FEATURES) * FEATURES * NODES
@@ -22,11 +23,11 @@ def tile_dyngraphsage_kernel(tc, x, w, offs, out):
     nc = tc.nc
     with (
         tc.tile_pool(name="held", bufs=1) as held,
-        tc.tile_pool(name="whole", bufs=2 * BLOCKS) as whole,
-        tc.tile_pool(name="sums", bufs=3 * BLOCKS) as sums,
+        tc.tile_pool(name="early", bufs=3 * BLOCKS) as early,
+        tc.tile_pool(name="late", bufs=3 * BLOCKS) as late,
         tc.tile_pool(name="means", bufs=2 * BLOCKS) as means,
         tc.tile_pool(name="staged", bufs=4) as staged,
-        tc.psum_pool(name="psum", bufs=2) as psum,
+        tc.psum_pool(name="psum", bufs=SPAN_CHUNKS) as psum,
     ):
         offsets = held.tile([P, NEIGHBOURS * NODES // PER_COLUMN], U16, name="offsets")
         nc.sync.dma_start(offsets[:], offs)
@@ -36,57 +37,69 @@ def tile_dyngraphsage_kernel(tc, x, w, offs, out):
         w_sb = held.tile([P, 2 * BLOCKS, FEATURES], BF16, name="w_sb")
         nc.sync.dma_start(w_sb[:], w.rearrange("(r p) e -> p r e", p=P))
 
-        zeros = held.tile([P, NODES], F32, name="zeros")
+        zeros = held.tile([P, SPAN], F32, name="zeros")
         nc.vector.memset(zeros[:], 0.0)
 
         x_bf = [held.tile([P, NODES], BF16, name=f"x_bf_{c}") for c in range(BLOCKS)]
         for c in range(BLOCKS):
             nc.scalar.activation(x_bf[c][:], x_f32[c][:], COPY)
 
-        totals = [zeros] * BLOCKS
-        for k in range(WHOLE):
-            first = k * NODES // PER_COLUMN
+        def add_neighbour(pool, k, first_node, width, totals):
+            first = (k * NODES + first_node) // PER_COLUMN
+            longer = []
             for c in range(BLOCKS):
-                picked = x_f32[c][:].indirect(offsets[:, first : first + NODES // PER_COLUMN])
-                longer = whole.tile([P, NODES], F32, name="longer_whole")
-                nc.vector.tensor_tensor(longer[:], picked, totals[c][:], ADD)
-                totals[c] = longer
+                picked = x_f32[c][:].indirect(offsets[:, first : first + width // PER_COLUMN])
+                total = pool.tile([P, width], F32, name="total")
+                nc.vector.tensor_tensor(total[:], picked, totals[c], ADD)
+                longer.append(total[:])
+            return longer
 
-        for j in range(CHUNKS):
-            nodes = slice(j * CHUNK, (j + 1) * CHUNK)
+        for span_start in range(0, NODES, SPAN):
+            chunk_starts = range(span_start, span_start + SPAN, CHUNK)
 
-            v = [psum.tile([P, CHUNK], F32, name=f"v{e}") for e in range(BLOCKS)]
-            for e in range(BLOCKS):
-                for c in range(BLOCKS):
-                    nc.tensor.matmul(
-                        v[e][:], w_sb[:, c, e * P : (e + 1) * P], x_bf[c][:, nodes], start=(c == 0), stop=False
-                    )
-
-            chunk_totals = [totals[c][:, nodes] for c in range(BLOCKS)]
-            for k in range(WHOLE, NEIGHBOURS):
-                first = (k * NODES + j * CHUNK) // PER_COLUMN
-                for c in range(BLOCKS):
-                    picked = x_f32[c][:].indirect(offsets[:, first : first + CHUNK // PER_COLUMN])
-                    longer = sums.tile([P, CHUNK], F32, name="longer")
-                    nc.vector.tensor_tensor(longer[:], picked, chunk_totals[c], ADD)
-                    chunk_totals[c] = longer[:]
-
-            for c in range(BLOCKS):
-                mean = means.tile([P, CHUNK], BF16, name="mean")
-                nc.scalar.activation(mean[:], chunk_totals[c], COPY, scale=1.0 / NEIGHBOURS)
+            v = {}
+            for chunk_start in chunk_starts:
                 for e in range(BLOCKS):
-                    nc.tensor.matmul(
-                        v[e][:], w_sb[:, BLOCKS + c, e * P : (e + 1) * P], mean[:], start=False, stop=(c == BLOCKS - 1)
-                    )
+                    v[chunk_start, e] = psum.tile([P, CHUNK], F32, name=f"v{e}")
+                    for c in range(BLOCKS):
+                        nc.tensor.matmul(
+                            v[chunk_start, e][:],
+                            w_sb[:, c, e * P : (e + 1) * P],
+                            x_bf[c][:, chunk_start : chunk_start + CHUNK],
+                            start=(c == 0),
+                            stop=False,
+                        )
 
-            for e in range(BLOCKS):
-                sloped = staged.tile([P, CHUNK], F32, name="sloped")
-                nc.scalar.activation(sloped[:], v[e][:], COPY, scale=SLOPE)
-                result = staged.tile([P, CHUNK], F32, name="result")
-                if j < CHUNKS - 1:
-                    lifted = staged.tile([P, CHUNK], F32, name="lifted")
-                    nc.scalar.activation(lifted[:], v[e][:], RELU, scale=1.0 - SLOPE)
-                    nc.gpsimd.tensor_tensor(result[:], sloped[:], lifted[:], ADD)
-                else:
-                    nc.vector.tensor_tensor(result[:], v[e][:], sloped[:], MAX)
-                nc.sync.dma_start(out[e * P : (e + 1) * P, nodes], result[:])
+            span_totals = [zeros[:]] * BLOCKS
+            for k in range(EARLY):
+                span_totals = add_neighbour(early, k, span_start, SPAN, span_totals)
+
+            for chunk_start in chunk_starts:
+                inside = slice(chunk_start - span_start, chunk_start - span_start + CHUNK)
+                totals = [total[:, inside] for total in span_totals]
+                for k in range(EARLY, NEIGHBOURS):
+                    totals = add_neighbour(late, k, chunk_start, CHUNK, totals)
+
+                for c in range(BLOCKS):
+                    mean = means.tile([P, CHUNK], BF16, name="mean")
+                    nc.scalar.activation(mean[:], totals[c], COPY, scale=1.0 / NEIGHBOURS)
+                    for e in range(BLOCKS):
+                        nc.tensor.matmul(
+                            v[chunk_start, e][:],
+                            w_sb[:, BLOCKS + c, e * P : (e + 1) * P],
+                            mean[:],
+                            start=False,
+                            stop=(c == BLOCKS - 1),
+                        )
+
+                for e in range(BLOCKS):
+                    sloped = staged.tile([P, CHUNK], F32, name="sloped")
+                    nc.scalar.activation(sloped[:], v[chunk_start, e][:], COPY, scale=SLOPE)
+                    result = staged.tile([P, CHUNK], F32, name="result")
+                    if chunk_start + CHUNK < NODES:
+                        lifted = staged.tile([P, CHUNK], F32, name="lifted")
+                        nc.scalar.activation(lifted[:], v[chunk_start, e][:], RELU, scale=1.0 - SLOPE)
+                        nc.gpsimd.tensor_tensor(result[:], sloped[:], lifted[:], ADD)
+                    else:
+                        nc.vector.tensor_tensor(result[:], v[chunk_start, e][:], sloped[:], MAX)
+                    nc.sync.dma_start(out[e * P : (e + 1) * P, chunk_start : chunk_start + CHUNK], result[:])

@@ -8,12 +8,11 @@ P = 128
 FEATURES = 512
 NODES = 2048
 NEIGHBOURS = 4
-EARLY = 2
+WHOLE = 1
 SLOPE = 0.2
 BLOCKS = FEATURES // P
 CHUNK = 512
-SPAN_CHUNKS = 8 // BLOCKS
-SPAN = SPAN_CHUNKS * CHUNK
+CHUNKS = NODES // CHUNK
 PER_COLUMN = 16
 
 FLOPS = 2 * (2 * FEATURES) * FEATURES * NODES
@@ -23,11 +22,11 @@ def tile_dyngraphsage_kernel(tc, x, w, offs, out):
     nc = tc.nc
     with (
         tc.tile_pool(name="held", bufs=1) as held,
-        tc.tile_pool(name="early", bufs=3 * BLOCKS) as early,
-        tc.tile_pool(name="late", bufs=3 * BLOCKS) as late,
-        tc.tile_pool(name="means", bufs=2 * BLOCKS) as means,
+        tc.tile_pool(name="whole", bufs=BLOCKS) as whole,
+        tc.tile_pool(name="sums", bufs=3 * BLOCKS) as sums,
+        tc.tile_pool(name="ring", bufs=BLOCKS) as ring,
         tc.tile_pool(name="staged", bufs=4) as staged,
-        tc.psum_pool(name="psum", bufs=SPAN_CHUNKS) as psum,
+        tc.psum_pool(name="psum", bufs=2) as psum,
     ):
         offsets = held.tile([P, NEIGHBOURS * NODES // PER_COLUMN], U16, name="offsets")
         nc.sync.dma_start(offsets[:], offs)
@@ -37,69 +36,57 @@ def tile_dyngraphsage_kernel(tc, x, w, offs, out):
         w_sb = held.tile([P, 2 * BLOCKS, FEATURES], BF16, name="w_sb")
         nc.sync.dma_start(w_sb[:], w.rearrange("(r p) e -> p r e", p=P))
 
-        zeros = held.tile([P, SPAN], F32, name="zeros")
+        zeros = held.tile([P, NODES], F32, name="zeros")
         nc.vector.memset(zeros[:], 0.0)
 
         x_bf = [held.tile([P, NODES], BF16, name=f"x_bf_{c}") for c in range(BLOCKS)]
         for c in range(BLOCKS):
             nc.scalar.activation(x_bf[c][:], x_f32[c][:], COPY)
 
-        def add_neighbour(pool, k, first_node, width, totals):
-            first = (k * NODES + first_node) // PER_COLUMN
-            longer = []
+        totals = [zeros] * BLOCKS
+        for k in range(WHOLE):
+            first = k * NODES // PER_COLUMN
             for c in range(BLOCKS):
-                picked = x_f32[c][:].indirect(offsets[:, first : first + width // PER_COLUMN])
-                total = pool.tile([P, width], F32, name="total")
-                nc.vector.tensor_tensor(total[:], picked, totals[c], ADD)
-                longer.append(total[:])
-            return longer
+                picked = x_f32[c][:].indirect(offsets[:, first : first + NODES // PER_COLUMN])
+                longer = whole.tile([P, NODES], F32, name="longer_whole")
+                nc.vector.tensor_tensor(longer[:], picked, totals[c][:], ADD)
+                totals[c] = longer
 
-        for span_start in range(0, NODES, SPAN):
-            chunk_starts = range(span_start, span_start + SPAN, CHUNK)
+        for j in range(CHUNKS):
+            nodes = slice(j * CHUNK, (j + 1) * CHUNK)
 
-            v = {}
-            for chunk_start in chunk_starts:
-                for e in range(BLOCKS):
-                    v[chunk_start, e] = psum.tile([P, CHUNK], F32, name=f"v{e}")
-                    for c in range(BLOCKS):
-                        nc.tensor.matmul(
-                            v[chunk_start, e][:],
-                            w_sb[:, c, e * P : (e + 1) * P],
-                            x_bf[c][:, chunk_start : chunk_start + CHUNK],
-                            start=(c == 0),
-                            stop=False,
-                        )
-
-            span_totals = [zeros[:]] * BLOCKS
-            for k in range(EARLY):
-                span_totals = add_neighbour(early, k, span_start, SPAN, span_totals)
-
-            for chunk_start in chunk_starts:
-                inside = slice(chunk_start - span_start, chunk_start - span_start + CHUNK)
-                totals = [total[:, inside] for total in span_totals]
-                for k in range(EARLY, NEIGHBOURS):
-                    totals = add_neighbour(late, k, chunk_start, CHUNK, totals)
-
+            v = [psum.tile([P, CHUNK], F32, name=f"v{e}") for e in range(BLOCKS)]
+            for e in range(BLOCKS):
                 for c in range(BLOCKS):
-                    mean = means.tile([P, CHUNK], BF16, name="mean")
-                    nc.scalar.activation(mean[:], totals[c], COPY, scale=1.0 / NEIGHBOURS)
-                    for e in range(BLOCKS):
-                        nc.tensor.matmul(
-                            v[chunk_start, e][:],
-                            w_sb[:, BLOCKS + c, e * P : (e + 1) * P],
-                            mean[:],
-                            start=False,
-                            stop=(c == BLOCKS - 1),
-                        )
+                    nc.tensor.matmul(
+                        v[e][:], w_sb[:, c, e * P : (e + 1) * P], x_bf[c][:, nodes], start=(c == 0), stop=False
+                    )
 
+            chunk_totals = [totals[c][:, nodes] for c in range(BLOCKS)]
+            for k in range(WHOLE, NEIGHBOURS):
+                first = (k * NODES + j * CHUNK) // PER_COLUMN
+                for c in range(BLOCKS):
+                    picked = x_f32[c][:].indirect(offsets[:, first : first + CHUNK // PER_COLUMN])
+                    longer = sums.tile([P, CHUNK], F32, name="longer")
+                    nc.vector.tensor_tensor(longer[:], picked, chunk_totals[c], ADD)
+                    chunk_totals[c] = longer[:]
+
+            for c in range(BLOCKS):
+                mean = ring.tile([P, CHUNK], BF16, name="mean", tag="ring")
+                nc.scalar.activation(mean[:], chunk_totals[c], COPY, scale=1.0 / NEIGHBOURS)
                 for e in range(BLOCKS):
-                    sloped = staged.tile([P, CHUNK], F32, name="sloped")
-                    nc.scalar.activation(sloped[:], v[chunk_start, e][:], COPY, scale=SLOPE)
-                    result = staged.tile([P, CHUNK], F32, name="result")
-                    if chunk_start + CHUNK < NODES:
-                        lifted = staged.tile([P, CHUNK], F32, name="lifted")
-                        nc.scalar.activation(lifted[:], v[chunk_start, e][:], RELU, scale=1.0 - SLOPE)
-                        nc.gpsimd.tensor_tensor(result[:], sloped[:], lifted[:], ADD)
-                    else:
-                        nc.vector.tensor_tensor(result[:], v[chunk_start, e][:], sloped[:], MAX)
-                    nc.sync.dma_start(out[e * P : (e + 1) * P, chunk_start : chunk_start + CHUNK], result[:])
+                    nc.tensor.matmul(
+                        v[e][:], w_sb[:, BLOCKS + c, e * P : (e + 1) * P], mean[:], start=False, stop=(c == BLOCKS - 1)
+                    )
+
+            for e in range(BLOCKS):
+                sloped = ring.tile([P, CHUNK], F32, name="sloped", tag="ring")
+                nc.scalar.activation(sloped[:], v[e][:], COPY, scale=SLOPE)
+                result = staged.tile([P, CHUNK], F32, name="result")
+                if j < CHUNKS - 1:
+                    lifted = ring.tile([P, CHUNK], F32, name="lifted", tag="ring")
+                    nc.scalar.activation(lifted[:], v[e][:], RELU, scale=1.0 - SLOPE)
+                    nc.gpsimd.tensor_tensor(result[:], sloped[:], lifted[:], ADD)
+                else:
+                    nc.vector.tensor_tensor(result[:], v[e][:], sloped[:], MAX)
+                nc.sync.dma_start(out[e * P : (e + 1) * P, nodes], result[:])

@@ -24,8 +24,8 @@ def tile_dyngraphsage_kernel(tc, x, w, offs, out):
         tc.tile_pool(name="held", bufs=1) as held,
         tc.tile_pool(name="whole", bufs=BLOCKS) as whole,
         tc.tile_pool(name="sums", bufs=3 * BLOCKS) as sums,
-        tc.tile_pool(name="ring", bufs=BLOCKS) as ring,
-        tc.tile_pool(name="staged", bufs=4) as staged,
+        tc.tile_pool(name="means", bufs=1) as means,
+        tc.tile_pool(name="staged", bufs=2 * BLOCKS) as staged,
         tc.psum_pool(name="psum", bufs=2) as psum,
     ):
         offsets = held.tile([P, NEIGHBOURS * NODES // PER_COLUMN], U16, name="offsets")
@@ -71,20 +71,24 @@ def tile_dyngraphsage_kernel(tc, x, w, offs, out):
                     nc.vector.tensor_tensor(longer[:], picked, chunk_totals[c], ADD)
                     chunk_totals[c] = longer[:]
 
+            mean = means.tile([P, BLOCKS, CHUNK], BF16, name="mean")
             for c in range(BLOCKS):
-                mean = ring.tile([P, CHUNK], BF16, name="mean", tag="ring")
-                nc.scalar.activation(mean[:], chunk_totals[c], COPY, scale=1.0 / NEIGHBOURS)
+                nc.scalar.activation(mean[:, c, :], chunk_totals[c], COPY, scale=1.0 / NEIGHBOURS)
                 for e in range(BLOCKS):
                     nc.tensor.matmul(
-                        v[e][:], w_sb[:, BLOCKS + c, e * P : (e + 1) * P], mean[:], start=False, stop=(c == BLOCKS - 1)
+                        v[e][:],
+                        w_sb[:, BLOCKS + c, e * P : (e + 1) * P],
+                        mean[:, c, :],
+                        start=False,
+                        stop=(c == BLOCKS - 1),
                     )
 
             for e in range(BLOCKS):
-                sloped = ring.tile([P, CHUNK], F32, name="sloped", tag="ring")
+                sloped = staged.tile([P, CHUNK], F32, name="sloped")
                 nc.scalar.activation(sloped[:], v[e][:], COPY, scale=SLOPE)
                 result = staged.tile([P, CHUNK], F32, name="result")
                 if j < CHUNKS - 1:
-                    lifted = ring.tile([P, CHUNK], F32, name="lifted", tag="ring")
+                    lifted = staged.tile([P, CHUNK], F32, name="lifted")
                     nc.scalar.activation(lifted[:], v[e][:], RELU, scale=1.0 - SLOPE)
                     nc.gpsimd.tensor_tensor(result[:], sloped[:], lifted[:], ADD)
                 else:

@@ -2,13 +2,13 @@ import concourse.mybir as mybir
 
 F32, BF16, U16 = mybir.dt.float32, mybir.dt.bfloat16, mybir.dt.uint16
 ADD, MAX = mybir.AluOpType.add, mybir.AluOpType.max
-COPY, RELU = mybir.ActivationFunctionType.Copy, mybir.ActivationFunctionType.Relu
+COPY = mybir.ActivationFunctionType.Copy
 
 P = 128
 FEATURES = 512
 NODES = 2048
 NEIGHBOURS = 4
-WHOLE = 1
+WHOLE = 2
 SLOPE = 0.2
 BLOCKS = FEATURES // P
 CHUNK = 512
@@ -22,10 +22,10 @@ def tile_dyngraphsage_kernel(tc, x, w, offs, out):
     nc = tc.nc
     with (
         tc.tile_pool(name="held", bufs=1) as held,
-        tc.tile_pool(name="whole", bufs=BLOCKS) as whole,
+        tc.tile_pool(name="whole", bufs=2 * BLOCKS) as whole,
         tc.tile_pool(name="sums", bufs=3 * BLOCKS) as sums,
         tc.tile_pool(name="means", bufs=1) as means,
-        tc.tile_pool(name="staged", bufs=2 * BLOCKS) as staged,
+        tc.tile_pool(name="staged", bufs=BLOCKS) as staged,
         tc.psum_pool(name="psum", bufs=2) as psum,
     ):
         offsets = held.tile([P, NEIGHBOURS * NODES // PER_COLUMN], U16, name="offsets")
@@ -87,10 +87,5 @@ def tile_dyngraphsage_kernel(tc, x, w, offs, out):
                 sloped = staged.tile([P, CHUNK], F32, name="sloped")
                 nc.scalar.activation(sloped[:], v[e][:], COPY, scale=SLOPE)
                 result = staged.tile([P, CHUNK], F32, name="result")
-                if j < CHUNKS - 1:
-                    lifted = staged.tile([P, CHUNK], F32, name="lifted")
-                    nc.scalar.activation(lifted[:], v[e][:], RELU, scale=1.0 - SLOPE)
-                    nc.gpsimd.tensor_tensor(result[:], sloped[:], lifted[:], ADD)
-                else:
-                    nc.vector.tensor_tensor(result[:], v[e][:], sloped[:], MAX)
+                nc.vector.tensor_tensor(result[:], v[e][:], sloped[:], MAX)
                 nc.sync.dma_start(out[e * P : (e + 1) * P, nodes], result[:])

@@ -1,18 +1,21 @@
 import concourse.mybir as mybir
+from concourse.masks import make_identity
 
 F32, BF16, U16 = mybir.dt.float32, mybir.dt.bfloat16, mybir.dt.uint16
 ADD, MAX = mybir.AluOpType.add, mybir.AluOpType.max
-COPY = mybir.ActivationFunctionType.Copy
+COPY, RELU = mybir.ActivationFunctionType.Copy, mybir.ActivationFunctionType.Relu
 
 P = 128
 FEATURES = 512
 NODES = 2048
 NEIGHBOURS = 4
-WHOLE = 2
 SLOPE = 0.2
 BLOCKS = FEATURES // P
 CHUNK = 512
 CHUNKS = NODES // CHUNK
+PAIR = 2 * CHUNK
+AHEAD = 2
+VECTOR_CHUNKS = 2
 PER_COLUMN = 16
 
 FLOPS = 2 * (2 * FEATURES) * FEATURES * NODES
@@ -22,11 +25,11 @@ def tile_dyngraphsage_kernel(tc, x, w, offs, out):
     nc = tc.nc
     with (
         tc.tile_pool(name="held", bufs=1) as held,
-        tc.tile_pool(name="whole", bufs=2 * BLOCKS) as whole,
+        tc.tile_pool(name="pairs", bufs=BLOCKS) as pairs,
         tc.tile_pool(name="sums", bufs=3 * BLOCKS) as sums,
-        tc.tile_pool(name="means", bufs=1) as means,
+        tc.tile_pool(name="moving", bufs=1) as moving,
         tc.tile_pool(name="staged", bufs=BLOCKS) as staged,
-        tc.psum_pool(name="psum", bufs=2) as psum,
+        tc.psum_pool(name="psum", bufs=AHEAD) as psum,
     ):
         offsets = held.tile([P, NEIGHBOURS * NODES // PER_COLUMN], U16, name="offsets")
         nc.sync.dma_start(offsets[:], offs)
@@ -36,44 +39,58 @@ def tile_dyngraphsage_kernel(tc, x, w, offs, out):
         w_sb = held.tile([P, 2 * BLOCKS, FEATURES], BF16, name="w_sb")
         nc.sync.dma_start(w_sb[:], w.rearrange("(r p) e -> p r e", p=P))
 
-        zeros = held.tile([P, NODES], F32, name="zeros")
+        zeros = held.tile([P, PAIR], F32, name="zeros")
         nc.vector.memset(zeros[:], 0.0)
+
+        plus = held.tile([P, P], F32, name="plus")
+        make_identity(nc, plus[:])
+        minus = held.tile([P, P], F32, name="minus")
+        nc.scalar.activation(minus[:], plus[:], COPY, scale=-1.0)
 
         x_bf = [held.tile([P, NODES], BF16, name=f"x_bf_{c}") for c in range(BLOCKS)]
         for c in range(BLOCKS):
             nc.scalar.activation(x_bf[c][:], x_f32[c][:], COPY)
 
-        totals = [zeros] * BLOCKS
-        for k in range(WHOLE):
-            first = k * NODES // PER_COLUMN
-            for c in range(BLOCKS):
-                picked = x_f32[c][:].indirect(offsets[:, first : first + NODES // PER_COLUMN])
-                longer = whole.tile([P, NODES], F32, name="longer_whole")
-                nc.vector.tensor_tensor(longer[:], picked, totals[c][:], ADD)
-                totals[c] = longer
-
-        for j in range(CHUNKS):
-            nodes = slice(j * CHUNK, (j + 1) * CHUNK)
-
+        def own_terms(j):
             v = [psum.tile([P, CHUNK], F32, name=f"v{e}") for e in range(BLOCKS)]
             for e in range(BLOCKS):
                 for c in range(BLOCKS):
                     nc.tensor.matmul(
-                        v[e][:], w_sb[:, c, e * P : (e + 1) * P], x_bf[c][:, nodes], start=(c == 0), stop=False
+                        v[e][:],
+                        w_sb[:, c, e * P : (e + 1) * P],
+                        x_bf[c][:, j * CHUNK : (j + 1) * CHUNK],
+                        start=(c == 0),
+                        stop=False,
                     )
+            return v
 
-            chunk_totals = [totals[c][:, nodes] for c in range(BLOCKS)]
-            for k in range(WHOLE, NEIGHBOURS):
+        banks = [own_terms(j) for j in range(AHEAD)]
+
+        for j in range(CHUNKS):
+            nodes = slice(j * CHUNK, (j + 1) * CHUNK)
+            v = banks[j]
+
+            if j * CHUNK % PAIR == 0:
+                first = j * CHUNK // PER_COLUMN
+                pair_totals = []
+                for c in range(BLOCKS):
+                    picked = x_f32[c][:].indirect(offsets[:, first : first + PAIR // PER_COLUMN])
+                    begun = pairs.tile([P, PAIR], F32, name="begun")
+                    nc.vector.tensor_tensor(begun[:], picked, zeros[:], ADD)
+                    pair_totals.append(begun)
+            within = slice(j * CHUNK % PAIR, j * CHUNK % PAIR + CHUNK)
+            totals = [pair_totals[c][:, within] for c in range(BLOCKS)]
+            for k in range(1, NEIGHBOURS):
                 first = (k * NODES + j * CHUNK) // PER_COLUMN
                 for c in range(BLOCKS):
                     picked = x_f32[c][:].indirect(offsets[:, first : first + CHUNK // PER_COLUMN])
                     longer = sums.tile([P, CHUNK], F32, name="longer")
-                    nc.vector.tensor_tensor(longer[:], picked, chunk_totals[c], ADD)
-                    chunk_totals[c] = longer[:]
+                    nc.vector.tensor_tensor(longer[:], picked, totals[c], ADD)
+                    totals[c] = longer[:]
 
-            mean = means.tile([P, BLOCKS, CHUNK], BF16, name="mean")
+            mean = moving.tile([P, BLOCKS, CHUNK], BF16, name="mean", tag="moving")
             for c in range(BLOCKS):
-                nc.scalar.activation(mean[:, c, :], chunk_totals[c], COPY, scale=1.0 / NEIGHBOURS)
+                nc.scalar.activation(mean[:, c, :], totals[c], COPY, scale=1.0 / NEIGHBOURS)
                 for e in range(BLOCKS):
                     nc.tensor.matmul(
                         v[e][:],
@@ -83,9 +100,23 @@ def tile_dyngraphsage_kernel(tc, x, w, offs, out):
                         stop=(c == BLOCKS - 1),
                     )
 
-            for e in range(BLOCKS):
-                sloped = staged.tile([P, CHUNK], F32, name="sloped")
-                nc.scalar.activation(sloped[:], v[e][:], COPY, scale=SLOPE)
-                result = staged.tile([P, CHUNK], F32, name="result")
-                nc.vector.tensor_tensor(result[:], v[e][:], sloped[:], MAX)
-                nc.sync.dma_start(out[e * P : (e + 1) * P, nodes], result[:])
+            if j < CHUNKS - VECTOR_CHUNKS:
+                halves = moving.tile([P, BLOCKS, 2, CHUNK], F32, name="halves", tag="moving")
+                for e in range(BLOCKS):
+                    nc.scalar.activation(halves[:, e, 0, :], v[e][:], RELU)
+                    nc.scalar.activation(halves[:, e, 1, :], v[e][:], RELU, scale=-SLOPE)
+                    nc.tensor.matmul(v[e][:], plus[:], halves[:, e, 0, :], start=True, stop=False)
+                    nc.tensor.matmul(v[e][:], minus[:], halves[:, e, 1, :], start=False, stop=True)
+                    result = staged.tile([P, CHUNK], F32, name="result")
+                    nc.scalar.activation(result[:], v[e][:], COPY)
+                    nc.sync.dma_start(out[e * P : (e + 1) * P, nodes], result[:])
+            else:
+                for e in range(BLOCKS):
+                    sloped = staged.tile([P, CHUNK], F32, name="sloped")
+                    nc.scalar.activation(sloped[:], v[e][:], COPY, scale=SLOPE)
+                    result = staged.tile([P, CHUNK], F32, name="result")
+                    nc.vector.tensor_tensor(result[:], v[e][:], sloped[:], MAX)
+                    nc.sync.dma_start(out[e * P : (e + 1) * P, nodes], result[:])
+
+            if j + AHEAD < CHUNKS:
+                banks.append(own_terms(j + AHEAD))

@@ -25,8 +25,8 @@ def tile_dyngraphsage_kernel(tc, x, w, offs, out):
     nc = tc.nc
     with (
         tc.tile_pool(name="held", bufs=1) as held,
-        tc.tile_pool(name="pairs", bufs=BLOCKS) as pairs,
-        tc.tile_pool(name="sums", bufs=3 * BLOCKS) as sums,
+        tc.tile_pool(name="pairs", bufs=2 * BLOCKS) as pairs,
+        tc.tile_pool(name="sums", bufs=5 * BLOCKS) as sums,
         tc.tile_pool(name="moving", bufs=1) as moving,
         tc.tile_pool(name="staged", bufs=BLOCKS) as staged,
         tc.psum_pool(name="psum", bufs=AHEAD) as psum,

@@ -13,9 +13,9 @@ SLOPE = 0.2
 BLOCKS = FEATURES // P
 CHUNK = 512
 CHUNKS = NODES // CHUNK
-PAIR = 2 * CHUNK
-AHEAD = 2
-VECTOR_CHUNKS = 2
+PAIR = 2
+PAIRS = CHUNKS // PAIR
+TOGETHER = (2, 2)
 PER_COLUMN = 16
 
 FLOPS = 2 * (2 * FEATURES) * FEATURES * NODES
@@ -25,11 +25,11 @@ def tile_dyngraphsage_kernel(tc, x, w, offs, out):
     nc = tc.nc
     with (
         tc.tile_pool(name="held", bufs=1) as held,
-        tc.tile_pool(name="pairs", bufs=2 * BLOCKS) as pairs,
+        tc.tile_pool(name="wide", bufs=2 * BLOCKS) as wide,
         tc.tile_pool(name="sums", bufs=5 * BLOCKS) as sums,
         tc.tile_pool(name="moving", bufs=1) as moving,
         tc.tile_pool(name="staged", bufs=BLOCKS) as staged,
-        tc.psum_pool(name="psum", bufs=AHEAD) as psum,
+        tc.psum_pool(name="psum", bufs=PAIR) as psum,
     ):
         offsets = held.tile([P, NEIGHBOURS * NODES // PER_COLUMN], U16, name="offsets")
         nc.sync.dma_start(offsets[:], offs)
@@ -39,7 +39,7 @@ def tile_dyngraphsage_kernel(tc, x, w, offs, out):
         w_sb = held.tile([P, 2 * BLOCKS, FEATURES], BF16, name="w_sb")
         nc.sync.dma_start(w_sb[:], w.rearrange("(r p) e -> p r e", p=P))
 
-        zeros = held.tile([P, PAIR], F32, name="zeros")
+        zeros = held.tile([P, PAIR * CHUNK], F32, name="zeros")
         nc.vector.memset(zeros[:], 0.0)
 
         plus = held.tile([P, P], F32, name="plus")
@@ -50,6 +50,16 @@ def tile_dyngraphsage_kernel(tc, x, w, offs, out):
         x_bf = [held.tile([P, NODES], BF16, name=f"x_bf_{c}") for c in range(BLOCKS)]
         for c in range(BLOCKS):
             nc.scalar.activation(x_bf[c][:], x_f32[c][:], COPY)
+
+        def add_neighbours(pool, k, start, count, totals):
+            first = (k * NODES + start) // PER_COLUMN
+            longer = []
+            for c in range(BLOCKS):
+                picked = x_f32[c][:].indirect(offsets[:, first : first + count // PER_COLUMN])
+                total = pool.tile([P, count], F32, name="total")
+                nc.vector.tensor_tensor(total[:], picked, totals[c], ADD)
+                longer.append(total[:])
+            return longer
 
         def own_terms(j):
             v = [psum.tile([P, CHUNK], F32, name=f"v{e}") for e in range(BLOCKS)]
@@ -64,59 +74,49 @@ def tile_dyngraphsage_kernel(tc, x, w, offs, out):
                     )
             return v
 
-        banks = [own_terms(j) for j in range(AHEAD)]
+        banks = [own_terms(j) for j in range(PAIR)]
 
-        for j in range(CHUNKS):
-            nodes = slice(j * CHUNK, (j + 1) * CHUNK)
-            v = banks[j]
+        for pair in range(PAIRS):
+            pair_totals = [zeros[:]] * BLOCKS
+            for k in range(TOGETHER[pair]):
+                pair_totals = add_neighbours(wide, k, pair * PAIR * CHUNK, PAIR * CHUNK, pair_totals)
 
-            if j * CHUNK % PAIR == 0:
-                first = j * CHUNK // PER_COLUMN
-                pair_totals = []
+            for j in range(pair * PAIR, (pair + 1) * PAIR):
+                nodes = slice(j * CHUNK, (j + 1) * CHUNK)
+                v = banks[j]
+
+                within = slice(j % PAIR * CHUNK, (j % PAIR + 1) * CHUNK)
+                totals = [pair_totals[c][:, within] for c in range(BLOCKS)]
+                for k in range(TOGETHER[pair], NEIGHBOURS):
+                    totals = add_neighbours(sums, k, j * CHUNK, CHUNK, totals)
+
+                mean = moving.tile([P, BLOCKS, CHUNK], BF16, name="mean", tag="moving")
                 for c in range(BLOCKS):
-                    picked = x_f32[c][:].indirect(offsets[:, first : first + PAIR // PER_COLUMN])
-                    begun = pairs.tile([P, PAIR], F32, name="begun")
-                    nc.vector.tensor_tensor(begun[:], picked, zeros[:], ADD)
-                    pair_totals.append(begun)
-            within = slice(j * CHUNK % PAIR, j * CHUNK % PAIR + CHUNK)
-            totals = [pair_totals[c][:, within] for c in range(BLOCKS)]
-            for k in range(1, NEIGHBOURS):
-                first = (k * NODES + j * CHUNK) // PER_COLUMN
-                for c in range(BLOCKS):
-                    picked = x_f32[c][:].indirect(offsets[:, first : first + CHUNK // PER_COLUMN])
-                    longer = sums.tile([P, CHUNK], F32, name="longer")
-                    nc.vector.tensor_tensor(longer[:], picked, totals[c], ADD)
-                    totals[c] = longer[:]
+                    nc.scalar.activation(mean[:, c, :], totals[c], COPY, scale=1.0 / NEIGHBOURS)
+                    for e in range(BLOCKS):
+                        nc.tensor.matmul(
+                            v[e][:],
+                            w_sb[:, BLOCKS + c, e * P : (e + 1) * P],
+                            mean[:, c, :],
+                            start=False,
+                            stop=(c == BLOCKS - 1),
+                        )
 
-            mean = moving.tile([P, BLOCKS, CHUNK], BF16, name="mean", tag="moving")
-            for c in range(BLOCKS):
-                nc.scalar.activation(mean[:, c, :], totals[c], COPY, scale=1.0 / NEIGHBOURS)
-                for e in range(BLOCKS):
-                    nc.tensor.matmul(
-                        v[e][:],
-                        w_sb[:, BLOCKS + c, e * P : (e + 1) * P],
-                        mean[:, c, :],
-                        start=False,
-                        stop=(c == BLOCKS - 1),
-                    )
-
-            if j < CHUNKS - VECTOR_CHUNKS:
-                halves = moving.tile([P, BLOCKS, 2, CHUNK], F32, name="halves", tag="moving")
-                for e in range(BLOCKS):
-                    nc.scalar.activation(halves[:, e, 0, :], v[e][:], RELU)
-                    nc.scalar.activation(halves[:, e, 1, :], v[e][:], RELU, scale=-SLOPE)
-                    nc.tensor.matmul(v[e][:], plus[:], halves[:, e, 0, :], start=True, stop=False)
-                    nc.tensor.matmul(v[e][:], minus[:], halves[:, e, 1, :], start=False, stop=True)
-                    result = staged.tile([P, CHUNK], F32, name="result")
-                    nc.scalar.activation(result[:], v[e][:], COPY)
-                    nc.sync.dma_start(out[e * P : (e + 1) * P, nodes], result[:])
-            else:
-                for e in range(BLOCKS):
-                    sloped = staged.tile([P, CHUNK], F32, name="sloped")
-                    nc.scalar.activation(sloped[:], v[e][:], COPY, scale=SLOPE)
-                    result = staged.tile([P, CHUNK], F32, name="result")
-                    nc.vector.tensor_tensor(result[:], v[e][:], sloped[:], MAX)
-                    nc.sync.dma_start(out[e * P : (e + 1) * P, nodes], result[:])
-
-            if j + AHEAD < CHUNKS:
-                banks.append(own_terms(j + AHEAD))
+                if pair < PAIRS - 1:
+                    halves = moving.tile([P, BLOCKS, 2, CHUNK], F32, name="halves", tag="moving")
+                    for e in range(BLOCKS):
+                        nc.scalar.activation(halves[:, e, 0, :], v[e][:], RELU)
+                        nc.scalar.activation(halves[:, e, 1, :], v[e][:], RELU, scale=-SLOPE)
+                        nc.tensor.matmul(v[e][:], plus[:], halves[:, e, 0, :], start=True, stop=False)
+                        nc.tensor.matmul(v[e][:], minus[:], halves[:, e, 1, :], start=False, stop=True)
+                        result = staged.tile([P, CHUNK], F32, name="result")
+                        nc.scalar.activation(result[:], v[e][:], COPY)
+                        nc.sync.dma_start(out[e * P : (e + 1) * P, nodes], result[:])
+                    banks.append(own_terms(j + PAIR))
+                else:
+                    for e in range(BLOCKS):
+                        sloped = staged.tile([P, CHUNK], F32, name="sloped")
+                        nc.scalar.activation(sloped[:], v[e][:], COPY, scale=SLOPE)
+                        result = staged.tile([P, CHUNK], F32, name="result")
+                        nc.vector.tensor_tensor(result[:], v[e][:], sloped[:], MAX)
+                        nc.sync.dma_start(out[e * P : (e + 1) * P, nodes], result[:])

@@ -16,6 +16,7 @@ CHUNKS = NODES // CHUNK
 PAIR = 2
 PAIRS = CHUNKS // PAIR
 TOGETHER = (2, 2)
+BY_TENSOR = (BLOCKS, BLOCKS, 1, 0)
 PER_COLUMN = 16
 
 FLOPS = 2 * (2 * FEATURES) * FEATURES * NODES
@@ -102,21 +103,24 @@ def tile_dyngraphsage_kernel(tc, x, w, offs, out):
                             stop=(c == BLOCKS - 1),
                         )
 
-                if pair < PAIRS - 1:
+                if BY_TENSOR[j] == BLOCKS:
                     halves = moving.tile([P, BLOCKS, 2, CHUNK], F32, name="halves", tag="moving")
-                    for e in range(BLOCKS):
-                        nc.scalar.activation(halves[:, e, 0, :], v[e][:], RELU)
-                        nc.scalar.activation(halves[:, e, 1, :], v[e][:], RELU, scale=-SLOPE)
-                        nc.tensor.matmul(v[e][:], plus[:], halves[:, e, 0, :], start=True, stop=False)
-                        nc.tensor.matmul(v[e][:], minus[:], halves[:, e, 1, :], start=False, stop=True)
-                        result = staged.tile([P, CHUNK], F32, name="result")
-                        nc.scalar.activation(result[:], v[e][:], COPY)
-                        nc.sync.dma_start(out[e * P : (e + 1) * P, nodes], result[:])
+                elif BY_TENSOR[j] > 0:
+                    halves = held.tile([P, BY_TENSOR[j], 2, CHUNK], F32, name="few_halves")
+                for e in range(BY_TENSOR[j]):
+                    nc.scalar.activation(halves[:, e, 0, :], v[e][:], RELU)
+                    nc.scalar.activation(halves[:, e, 1, :], v[e][:], RELU, scale=-SLOPE)
+                    nc.tensor.matmul(v[e][:], plus[:], halves[:, e, 0, :], start=True, stop=False)
+                    nc.tensor.matmul(v[e][:], minus[:], halves[:, e, 1, :], start=False, stop=True)
+                    result = staged.tile([P, CHUNK], F32, name="result")
+                    nc.scalar.activation(result[:], v[e][:], COPY)
+                    nc.sync.dma_start(out[e * P : (e + 1) * P, nodes], result[:])
+                for e in range(BY_TENSOR[j], BLOCKS):
+                    sloped = staged.tile([P, CHUNK], F32, name="sloped")
+                    nc.scalar.activation(sloped[:], v[e][:], COPY, scale=SLOPE)
+                    result = staged.tile([P, CHUNK], F32, name="result")
+                    nc.vector.tensor_tensor(result[:], v[e][:], sloped[:], MAX)
+                    nc.sync.dma_start(out[e * P : (e + 1) * P, nodes], result[:])
+
+                if j + PAIR < CHUNKS:
                     banks.append(own_terms(j + PAIR))
-                else:
-                    for e in range(BLOCKS):
-                        sloped = staged.tile([P, CHUNK], F32, name="sloped")
-                        nc.scalar.activation(sloped[:], v[e][:], COPY, scale=SLOPE)
-                        result = staged.tile([P, CHUNK], F32, name="result")
-                        nc.vector.tensor_tensor(result[:], v[e][:], sloped[:], MAX)
-                        nc.sync.dma_start(out[e * P : (e + 1) * P, nodes], result[:])

@@ -16,8 +16,11 @@ CHUNKS = NODES // CHUNK
 PAIR = 2
 PAIRS = CHUNKS // PAIR
 TOGETHER = (2, 2)
-BY_TENSOR = (BLOCKS, BLOCKS, 1, 0)
+BY_TENSOR = (BLOCKS, BLOCKS, 1)
 PER_COLUMN = 16
+HALF = CHUNK // 2
+WIDTHS = [CHUNK] * (CHUNKS - 1) + [HALF] * 2
+UNITS = [slice(sum(WIDTHS[:u]), sum(WIDTHS[: u + 1])) for u in range(len(WIDTHS))]
 
 FLOPS = 2 * (2 * FEATURES) * FEATURES * NODES
 
@@ -30,6 +33,7 @@ def tile_dyngraphsage_kernel(tc, x, w, offs, out):
         tc.tile_pool(name="sums", bufs=5 * BLOCKS) as sums,
         tc.tile_pool(name="moving", bufs=1) as moving,
         tc.tile_pool(name="staged", bufs=BLOCKS) as staged,
+        tc.tile_pool(name="results", bufs=3 * BLOCKS) as results,
         tc.psum_pool(name="psum", bufs=PAIR) as psum,
     ):
         offsets = held.tile([P, NEIGHBOURS * NODES // PER_COLUMN], U16, name="offsets")
@@ -62,20 +66,40 @@ def tile_dyngraphsage_kernel(tc, x, w, offs, out):
                 longer.append(total[:])
             return longer
 
-        def own_terms(j):
-            v = [psum.tile([P, CHUNK], F32, name=f"v{e}") for e in range(BLOCKS)]
+        def own_terms(nodes):
+            v = [psum.tile([P, nodes.stop - nodes.start], F32, name=f"v{e}") for e in range(BLOCKS)]
             for e in range(BLOCKS):
                 for c in range(BLOCKS):
                     nc.tensor.matmul(
                         v[e][:],
                         w_sb[:, c, e * P : (e + 1) * P],
-                        x_bf[c][:, j * CHUNK : (j + 1) * CHUNK],
+                        x_bf[c][:, nodes],
                         start=(c == 0),
                         stop=False,
                     )
             return v
 
-        banks = [own_terms(j) for j in range(PAIR)]
+        def mean_terms(v, mean, totals):
+            for c in range(BLOCKS):
+                nc.scalar.activation(mean[:, c, :], totals[c], COPY, scale=1.0 / NEIGHBOURS)
+                for e in range(BLOCKS):
+                    nc.tensor.matmul(
+                        v[e][:],
+                        w_sb[:, BLOCKS + c, e * P : (e + 1) * P],
+                        mean[:, c, :],
+                        start=False,
+                        stop=(c == BLOCKS - 1),
+                    )
+
+        def maximum(e, nodes, bank, plain):
+            width = nodes.stop - nodes.start
+            sloped = results.tile([P, width], F32, name="sloped")
+            nc.scalar.activation(sloped[:], bank, COPY, scale=SLOPE)
+            result = results.tile([P, width], F32, name="result")
+            nc.vector.tensor_tensor(result[:], plain, sloped[:], MAX)
+            nc.sync.dma_start(out[e * P : (e + 1) * P, nodes], result[:])
+
+        banks = [own_terms(nodes) for nodes in UNITS[:PAIR]]
 
         for pair in range(PAIRS):
             pair_totals = [zeros[:]] * BLOCKS
@@ -83,44 +107,44 @@ def tile_dyngraphsage_kernel(tc, x, w, offs, out):
                 pair_totals = add_neighbours(wide, k, pair * PAIR * CHUNK, PAIR * CHUNK, pair_totals)
 
             for j in range(pair * PAIR, (pair + 1) * PAIR):
-                nodes = slice(j * CHUNK, (j + 1) * CHUNK)
-                v = banks[j]
-
                 within = slice(j % PAIR * CHUNK, (j % PAIR + 1) * CHUNK)
                 totals = [pair_totals[c][:, within] for c in range(BLOCKS)]
+                if j == CHUNKS - 1:
+                    break
                 for k in range(TOGETHER[pair], NEIGHBOURS):
                     totals = add_neighbours(sums, k, j * CHUNK, CHUNK, totals)
 
+                v = banks[j]
                 mean = moving.tile([P, BLOCKS, CHUNK], BF16, name="mean", tag="moving")
-                for c in range(BLOCKS):
-                    nc.scalar.activation(mean[:, c, :], totals[c], COPY, scale=1.0 / NEIGHBOURS)
-                    for e in range(BLOCKS):
-                        nc.tensor.matmul(
-                            v[e][:],
-                            w_sb[:, BLOCKS + c, e * P : (e + 1) * P],
-                            mean[:, c, :],
-                            start=False,
-                            stop=(c == BLOCKS - 1),
-                        )
+                mean_terms(v, mean, totals)
 
                 if BY_TENSOR[j] == BLOCKS:
                     halves = moving.tile([P, BLOCKS, 2, CHUNK], F32, name="halves", tag="moving")
-                elif BY_TENSOR[j] > 0:
-                    halves = held.tile([P, BY_TENSOR[j], 2, CHUNK], F32, name="few_halves")
+                else:
+                    halves = moving.tile([P, BY_TENSOR[j], 2, CHUNK], F32, name="few_halves", tag="last")
                 for e in range(BY_TENSOR[j]):
                     nc.scalar.activation(halves[:, e, 0, :], v[e][:], RELU)
                     nc.scalar.activation(halves[:, e, 1, :], v[e][:], RELU, scale=-SLOPE)
                     nc.tensor.matmul(v[e][:], plus[:], halves[:, e, 0, :], start=True, stop=False)
                     nc.tensor.matmul(v[e][:], minus[:], halves[:, e, 1, :], start=False, stop=True)
-                    result = staged.tile([P, CHUNK], F32, name="result")
+                    result = results.tile([P, CHUNK], F32, name="result")
                     nc.scalar.activation(result[:], v[e][:], COPY)
-                    nc.sync.dma_start(out[e * P : (e + 1) * P, nodes], result[:])
+                    nc.sync.dma_start(out[e * P : (e + 1) * P, UNITS[j]], result[:])
                 for e in range(BY_TENSOR[j], BLOCKS):
-                    sloped = staged.tile([P, CHUNK], F32, name="sloped")
-                    nc.scalar.activation(sloped[:], v[e][:], COPY, scale=SLOPE)
-                    result = staged.tile([P, CHUNK], F32, name="result")
-                    nc.vector.tensor_tensor(result[:], v[e][:], sloped[:], MAX)
-                    nc.sync.dma_start(out[e * P : (e + 1) * P, nodes], result[:])
+                    plain = staged.tile([P, CHUNK], F32, name="plain")
+                    nc.scalar.activation(plain[:], v[e][:], COPY)
+                    maximum(e, UNITS[j], v[e][:], plain[:])
 
-                if j + PAIR < CHUNKS:
-                    banks.append(own_terms(j + PAIR))
+                banks.append(own_terms(UNITS[j + PAIR]))
+
+        totals = add_neighbours(sums, NEIGHBOURS - 2, (CHUNKS - 1) * CHUNK, CHUNK, totals)
+        for h in range(2):
+            nodes = UNITS[CHUNKS - 1 + h]
+            within = slice(h * HALF, (h + 1) * HALF)
+            half_totals = [totals[c][:, within] for c in range(BLOCKS)]
+            half_totals = add_neighbours(sums, NEIGHBOURS - 1, nodes.start, HALF, half_totals)
+            mean = moving.tile([P, BLOCKS, HALF], BF16, name="half_mean", tag=("moving", "last")[h])
+            v = banks[CHUNKS - 1 + h]
+            mean_terms(v, mean, half_totals)
+            for e in range(BLOCKS):
+                maximum(e, nodes, v[e][:], v[e][:])

@@ -12,15 +12,9 @@ NEIGHBOURS = 4
 SLOPE = 0.2
 BLOCKS = FEATURES // P
 CHUNK = 512
-CHUNKS = NODES // CHUNK
-PAIR = 2
-PAIRS = CHUNKS // PAIR
-TOGETHER = (2, 2)
-BY_TENSOR = (BLOCKS, BLOCKS, 1)
+PARTS = CHUNK // P
+PAIR = 2 * CHUNK
 PER_COLUMN = 16
-HALF = CHUNK // 2
-WIDTHS = [CHUNK] * (CHUNKS - 1) + [HALF] * 2
-UNITS = [slice(sum(WIDTHS[:u]), sum(WIDTHS[: u + 1])) for u in range(len(WIDTHS))]
 
 FLOPS = 2 * (2 * FEATURES) * FEATURES * NODES
 
@@ -29,12 +23,12 @@ def tile_dyngraphsage_kernel(tc, x, w, offs, out):
     nc = tc.nc
     with (
         tc.tile_pool(name="held", bufs=1) as held,
-        tc.tile_pool(name="wide", bufs=2 * BLOCKS) as wide,
-        tc.tile_pool(name="sums", bufs=5 * BLOCKS) as sums,
+        tc.tile_pool(name="wide", bufs=3 * BLOCKS) as wide,
+        tc.tile_pool(name="sums", bufs=3 * BLOCKS) as sums,
         tc.tile_pool(name="moving", bufs=1) as moving,
-        tc.tile_pool(name="staged", bufs=BLOCKS) as staged,
-        tc.tile_pool(name="results", bufs=3 * BLOCKS) as results,
-        tc.psum_pool(name="psum", bufs=PAIR) as psum,
+        tc.tile_pool(name="results", bufs=2) as results,
+        tc.tile_pool(name="last", bufs=BLOCKS) as last,
+        tc.psum_pool(name="products", bufs=2 * PARTS) as products,
     ):
         offsets = held.tile([P, NEIGHBOURS * NODES // PER_COLUMN], U16, name="offsets")
         nc.sync.dma_start(offsets[:], offs)
@@ -44,13 +38,10 @@ def tile_dyngraphsage_kernel(tc, x, w, offs, out):
         w_sb = held.tile([P, 2 * BLOCKS, FEATURES], BF16, name="w_sb")
         nc.sync.dma_start(w_sb[:], w.rearrange("(r p) e -> p r e", p=P))
 
-        zeros = held.tile([P, PAIR * CHUNK], F32, name="zeros")
+        zeros = held.tile([P, PAIR], F32, name="zeros")
         nc.vector.memset(zeros[:], 0.0)
-
-        plus = held.tile([P, P], F32, name="plus")
-        make_identity(nc, plus[:])
-        minus = held.tile([P, P], F32, name="minus")
-        nc.scalar.activation(minus[:], plus[:], COPY, scale=-1.0)
+        identity = held.tile([P, P], F32, name="identity")
+        make_identity(nc, identity[:])
 
         x_bf = [held.tile([P, NODES], BF16, name=f"x_bf_{c}") for c in range(BLOCKS)]
         for c in range(BLOCKS):
@@ -66,85 +57,104 @@ def tile_dyngraphsage_kernel(tc, x, w, offs, out):
                 longer.append(total[:])
             return longer
 
-        def own_terms(nodes):
-            v = [psum.tile([P, nodes.stop - nodes.start], F32, name=f"v{e}") for e in range(BLOCKS)]
+        out_by_row = out.rearrange("(e p) n -> p e n", p=P)
+
+        def part(b):
+            return slice(b * P, (b + 1) * P)
+
+        def open_turned(start):
+            v = [products.tile([P, FEATURES], F32, name="v") for b in range(PARTS)]
+            for b in range(PARTS):
+                own = slice(start + b * P, start + (b + 1) * P)
+                for c in range(BLOCKS):
+                    nc.tensor.matmul(v[b][:], x_bf[c][:, own], w_sb[:, c, :], start=(c == 0), stop=False)
+            return v
+
+        def open_straight(start):
+            v = [products.tile([P, CHUNK], F32, name="v") for e in range(BLOCKS)]
             for e in range(BLOCKS):
                 for c in range(BLOCKS):
                     nc.tensor.matmul(
                         v[e][:],
-                        w_sb[:, c, e * P : (e + 1) * P],
-                        x_bf[c][:, nodes],
+                        w_sb[:, c, part(e)],
+                        x_bf[c][:, start : start + CHUNK],
                         start=(c == 0),
                         stop=False,
                     )
             return v
 
-        def mean_terms(v, mean, totals):
+        def close_turned(v, totals):
+            mean = moving.tile([P, BLOCKS, CHUNK], BF16, name="mean", tag=f"buffer_{PARTS - 1}")
             for c in range(BLOCKS):
                 nc.scalar.activation(mean[:, c, :], totals[c], COPY, scale=1.0 / NEIGHBOURS)
-                for e in range(BLOCKS):
+                for b in range(PARTS):
                     nc.tensor.matmul(
-                        v[e][:],
-                        w_sb[:, BLOCKS + c, e * P : (e + 1) * P],
-                        mean[:, c, :],
+                        v[b][:],
+                        mean[:, c, part(b)],
+                        w_sb[:, BLOCKS + c, :],
                         start=False,
                         stop=(c == BLOCKS - 1),
                     )
 
-        def maximum(e, nodes, bank, plain):
-            width = nodes.stop - nodes.start
-            sloped = results.tile([P, width], F32, name="sloped")
-            nc.scalar.activation(sloped[:], bank, COPY, scale=SLOPE)
-            result = results.tile([P, width], F32, name="result")
-            nc.vector.tensor_tensor(result[:], plain, sloped[:], MAX)
-            nc.sync.dma_start(out[e * P : (e + 1) * P, nodes], result[:])
+        def finish_turned(v, start, copy):
+            result = results.tile([P, BLOCKS, CHUNK], F32, name="result")
+            for b in range(PARTS):
+                terms = moving.tile([P, 2, FEATURES], F32, name="terms", tag=f"buffer_{b}")
+                nc.scalar.activation(terms[:, 0, :], v[b][:], COPY)
+                nc.scalar.activation(terms[:, 1, :], v[b][:], RELU, scale=SLOPE - 1.0)
+                for e in range(BLOCKS):
+                    for t in range(2):
+                        nc.tensor.matmul(
+                            v[b][:, part(e)],
+                            terms[:, t, part(e)],
+                            identity[:],
+                            is_transpose=True,
+                            start=(t == 0),
+                            stop=(t == 1),
+                        )
+                copy(result[:, :, part(b)], v[b][:].rearrange("p (e n) -> p e n", e=BLOCKS))
+                if b % 2 == 1:
+                    two = slice((b - 1) * P, (b + 1) * P)
+                    nc.sync.dma_start(out_by_row[:, :, start + two.start : start + two.stop], result[:, :, two])
 
-        banks = [own_terms(nodes) for nodes in UNITS[:PAIR]]
+        totals = [zeros[:]] * BLOCKS
+        for k in range(NEIGHBOURS):
+            totals = add_neighbours(wide, k, 0, PAIR, totals)
+        banks_0, banks_1 = open_turned(0), open_turned(CHUNK)
+        close_turned(banks_0, [totals[c][:, 0:CHUNK] for c in range(BLOCKS)])
+        finish_turned(banks_0, 0, nc.scalar.copy)
+        banks_2 = open_turned(PAIR)
+        close_turned(banks_1, [totals[c][:, CHUNK:PAIR] for c in range(BLOCKS)])
+        finish_turned(banks_1, CHUNK, nc.scalar.copy)
+        banks_3 = open_straight(PAIR + CHUNK)
 
-        for pair in range(PAIRS):
-            pair_totals = [zeros[:]] * BLOCKS
-            for k in range(TOGETHER[pair]):
-                pair_totals = add_neighbours(wide, k, pair * PAIR * CHUNK, PAIR * CHUNK, pair_totals)
+        pair_totals = [zeros[:]] * BLOCKS
+        for k in range(NEIGHBOURS // 2):
+            pair_totals = add_neighbours(wide, k, PAIR, PAIR, pair_totals)
+        totals = [pair_totals[c][:, 0:CHUNK] for c in range(BLOCKS)]
+        for k in range(NEIGHBOURS // 2, NEIGHBOURS):
+            totals = add_neighbours(sums, k, PAIR, CHUNK, totals)
+        close_turned(banks_2, totals)
+        finish_turned(banks_2, PAIR, nc.vector.tensor_copy)
 
-            for j in range(pair * PAIR, (pair + 1) * PAIR):
-                within = slice(j % PAIR * CHUNK, (j % PAIR + 1) * CHUNK)
-                totals = [pair_totals[c][:, within] for c in range(BLOCKS)]
-                if j == CHUNKS - 1:
-                    break
-                for k in range(TOGETHER[pair], NEIGHBOURS):
-                    totals = add_neighbours(sums, k, j * CHUNK, CHUNK, totals)
-
-                v = banks[j]
-                mean = moving.tile([P, BLOCKS, CHUNK], BF16, name="mean", tag="moving")
-                mean_terms(v, mean, totals)
-
-                if BY_TENSOR[j] == BLOCKS:
-                    halves = moving.tile([P, BLOCKS, 2, CHUNK], F32, name="halves", tag="moving")
-                else:
-                    halves = moving.tile([P, BY_TENSOR[j], 2, CHUNK], F32, name="few_halves", tag="last")
-                for e in range(BY_TENSOR[j]):
-                    nc.scalar.activation(halves[:, e, 0, :], v[e][:], RELU)
-                    nc.scalar.activation(halves[:, e, 1, :], v[e][:], RELU, scale=-SLOPE)
-                    nc.tensor.matmul(v[e][:], plus[:], halves[:, e, 0, :], start=True, stop=False)
-                    nc.tensor.matmul(v[e][:], minus[:], halves[:, e, 1, :], start=False, stop=True)
-                    result = results.tile([P, CHUNK], F32, name="result")
-                    nc.scalar.activation(result[:], v[e][:], COPY)
-                    nc.sync.dma_start(out[e * P : (e + 1) * P, UNITS[j]], result[:])
-                for e in range(BY_TENSOR[j], BLOCKS):
-                    plain = staged.tile([P, CHUNK], F32, name="plain")
-                    nc.scalar.activation(plain[:], v[e][:], COPY)
-                    maximum(e, UNITS[j], v[e][:], plain[:])
-
-                banks.append(own_terms(UNITS[j + PAIR]))
-
-        totals = add_neighbours(sums, NEIGHBOURS - 2, (CHUNKS - 1) * CHUNK, CHUNK, totals)
-        for h in range(2):
-            nodes = UNITS[CHUNKS - 1 + h]
-            within = slice(h * HALF, (h + 1) * HALF)
-            half_totals = [totals[c][:, within] for c in range(BLOCKS)]
-            half_totals = add_neighbours(sums, NEIGHBOURS - 1, nodes.start, HALF, half_totals)
-            mean = moving.tile([P, BLOCKS, HALF], BF16, name="half_mean", tag=("moving", "last")[h])
-            v = banks[CHUNKS - 1 + h]
-            mean_terms(v, mean, half_totals)
+        start = PAIR + CHUNK
+        totals = [pair_totals[c][:, CHUNK:PAIR] for c in range(BLOCKS)]
+        for k in range(NEIGHBOURS // 2, NEIGHBOURS):
+            totals = add_neighbours(sums, k, start, CHUNK, totals)
+        mean = moving.tile([P, BLOCKS, CHUNK], BF16, name="mean", tag=f"buffer_{PARTS - 1}")
+        for c in range(BLOCKS):
+            nc.scalar.activation(mean[:, c, :], totals[c], COPY, scale=1.0 / NEIGHBOURS)
             for e in range(BLOCKS):
-                maximum(e, nodes, v[e][:], v[e][:])
+                nc.tensor.matmul(
+                    banks_3[e][:],
+                    w_sb[:, BLOCKS + c, part(e)],
+                    mean[:, c, :],
+                    start=False,
+                    stop=(c == BLOCKS - 1),
+                )
+        for e in range(BLOCKS):
+            sloped = last.tile([P, CHUNK], F32, name="sloped")
+            nc.scalar.activation(sloped[:], banks_3[e][:], COPY, scale=SLOPE)
+            largest = last.tile([P, CHUNK], F32, name="largest")
+            nc.vector.tensor_tensor(largest[:], banks_3[e][:], sloped[:], MAX)
+            nc.sync.dma_start(out[part(e), start : start + CHUNK], largest[:])

@@ -27,7 +27,7 @@ def tile_dyngraphsage_kernel(tc, x, w, offs, out):
         tc.tile_pool(name="sums", bufs=3 * BLOCKS) as sums,
         tc.tile_pool(name="moving", bufs=1) as moving,
         tc.tile_pool(name="results", bufs=2) as results,
-        tc.tile_pool(name="last", bufs=BLOCKS) as last,
+        tc.tile_pool(name="last", bufs=2 * BLOCKS) as last,
         tc.psum_pool(name="products", bufs=2 * PARTS) as products,
     ):
         offsets = held.tile([P, NEIGHBOURS * NODES // PER_COLUMN], U16, name="offsets")
@@ -96,7 +96,7 @@ def tile_dyngraphsage_kernel(tc, x, w, offs, out):
                         stop=(c == BLOCKS - 1),
                     )
 
-        def finish_turned(v, start, copy):
+        def finish_turned(v, start):
             result = results.tile([P, BLOCKS, CHUNK], F32, name="result")
             for b in range(PARTS):
                 terms = moving.tile([P, 2, FEATURES], F32, name="terms", tag=f"buffer_{b}")
@@ -112,49 +112,45 @@ def tile_dyngraphsage_kernel(tc, x, w, offs, out):
                             start=(t == 0),
                             stop=(t == 1),
                         )
-                copy(result[:, :, part(b)], v[b][:].rearrange("p (e n) -> p e n", e=BLOCKS))
+                nc.scalar.copy(result[:, :, part(b)], v[b][:].rearrange("p (e n) -> p e n", e=BLOCKS))
                 if b % 2 == 1:
                     two = slice((b - 1) * P, (b + 1) * P)
                     nc.sync.dma_start(out_by_row[:, :, start + two.start : start + two.stop], result[:, :, two])
 
+        def close_straight(banks, start, totals):
+            mean = moving.tile([P, BLOCKS, CHUNK], BF16, name="mean", tag=f"buffer_{PARTS - 1}")
+            for c in range(BLOCKS):
+                nc.scalar.activation(mean[:, c, :], totals[c], COPY, scale=1.0 / NEIGHBOURS)
+                for e in range(BLOCKS):
+                    nc.tensor.matmul(
+                        banks[e][:],
+                        w_sb[:, BLOCKS + c, part(e)],
+                        mean[:, c, :],
+                        start=False,
+                        stop=(c == BLOCKS - 1),
+                    )
+            for e in range(BLOCKS):
+                sloped = last.tile([P, CHUNK], F32, name="sloped")
+                nc.scalar.activation(sloped[:], banks[e][:], COPY, scale=SLOPE)
+                largest = last.tile([P, CHUNK], F32, name="largest")
+                nc.vector.tensor_tensor(largest[:], banks[e][:], sloped[:], MAX)
+                nc.sync.dma_start(out[part(e), start : start + CHUNK], largest[:])
+
         totals = [zeros[:]] * BLOCKS
         for k in range(NEIGHBOURS):
             totals = add_neighbours(wide, k, 0, PAIR, totals)
-        banks_0, banks_1 = open_turned(0), open_turned(CHUNK)
-        close_turned(banks_0, [totals[c][:, 0:CHUNK] for c in range(BLOCKS)])
-        finish_turned(banks_0, 0, nc.scalar.copy)
-        banks_2 = open_turned(PAIR)
-        close_turned(banks_1, [totals[c][:, CHUNK:PAIR] for c in range(BLOCKS)])
-        finish_turned(banks_1, CHUNK, nc.scalar.copy)
-        banks_3 = open_straight(PAIR + CHUNK)
+        banks = [open_turned(0), open_turned(CHUNK)]
+        for j in range(2):
+            close_turned(banks[j], [totals[c][:, j * CHUNK : (j + 1) * CHUNK] for c in range(BLOCKS)])
+            finish_turned(banks[j], j * CHUNK)
+            banks.append(open_straight(PAIR + j * CHUNK))
 
         pair_totals = [zeros[:]] * BLOCKS
         for k in range(NEIGHBOURS // 2):
             pair_totals = add_neighbours(wide, k, PAIR, PAIR, pair_totals)
-        totals = [pair_totals[c][:, 0:CHUNK] for c in range(BLOCKS)]
-        for k in range(NEIGHBOURS // 2, NEIGHBOURS):
-            totals = add_neighbours(sums, k, PAIR, CHUNK, totals)
-        close_turned(banks_2, totals)
-        finish_turned(banks_2, PAIR, nc.vector.tensor_copy)
-
-        start = PAIR + CHUNK
-        totals = [pair_totals[c][:, CHUNK:PAIR] for c in range(BLOCKS)]
-        for k in range(NEIGHBOURS // 2, NEIGHBOURS):
-            totals = add_neighbours(sums, k, start, CHUNK, totals)
-        mean = moving.tile([P, BLOCKS, CHUNK], BF16, name="mean", tag=f"buffer_{PARTS - 1}")
-        for c in range(BLOCKS):
-            nc.scalar.activation(mean[:, c, :], totals[c], COPY, scale=1.0 / NEIGHBOURS)
-            for e in range(BLOCKS):
-                nc.tensor.matmul(
-                    banks_3[e][:],
-                    w_sb[:, BLOCKS + c, part(e)],
-                    mean[:, c, :],
-                    start=False,
-                    stop=(c == BLOCKS - 1),
-                )
-        for e in range(BLOCKS):
-            sloped = last.tile([P, CHUNK], F32, name="sloped")
-            nc.scalar.activation(sloped[:], banks_3[e][:], COPY, scale=SLOPE)
-            largest = last.tile([P, CHUNK], F32, name="largest")
-            nc.vector.tensor_tensor(largest[:], banks_3[e][:], sloped[:], MAX)
-            nc.sync.dma_start(out[part(e), start : start + CHUNK], largest[:])
+        for j in range(2):
+            start = PAIR + j * CHUNK
+            totals = [pair_totals[c][:, j * CHUNK : (j + 1) * CHUNK] for c in range(BLOCKS)]
+            for k in range(NEIGHBOURS // 2, NEIGHBOURS):
+                totals = add_neighbours(sums, k, start, CHUNK, totals)
+            close_straight(banks[2 + j], start, totals)

@@ -42,6 +42,8 @@ def tile_dyngraphsage_kernel(tc, x, w, offs, out):
         nc.vector.memset(zeros[:], 0.0)
         identity = held.tile([P, P], F32, name="identity")
         make_identity(nc, identity[:])
+        minus = held.tile([P, P], F32, name="minus")
+        nc.scalar.activation(minus[:], identity[:], COPY, scale=-1.0)
 
         x_bf = [held.tile([P, NODES], BF16, name=f"x_bf_{c}") for c in range(BLOCKS)]
         for c in range(BLOCKS):
@@ -117,7 +119,7 @@ def tile_dyngraphsage_kernel(tc, x, w, offs, out):
                     two = slice((b - 1) * P, (b + 1) * P)
                     nc.sync.dma_start(out_by_row[:, :, start + two.start : start + two.stop], result[:, :, two])
 
-        def close_straight(banks, start, totals):
+        def close_straight(banks, totals):
             mean = moving.tile([P, BLOCKS, CHUNK], BF16, name="mean", tag=f"buffer_{PARTS - 1}")
             for c in range(BLOCKS):
                 nc.scalar.activation(mean[:, c, :], totals[c], COPY, scale=1.0 / NEIGHBOURS)
@@ -129,12 +131,22 @@ def tile_dyngraphsage_kernel(tc, x, w, offs, out):
                         start=False,
                         stop=(c == BLOCKS - 1),
                     )
-            for e in range(BLOCKS):
-                sloped = last.tile([P, CHUNK], F32, name="sloped")
-                nc.scalar.activation(sloped[:], banks[e][:], COPY, scale=SLOPE)
-                largest = last.tile([P, CHUNK], F32, name="largest")
-                nc.vector.tensor_tensor(largest[:], banks[e][:], sloped[:], MAX)
-                nc.sync.dma_start(out[part(e), start : start + CHUNK], largest[:])
+        def finish_by_tensor(bank, e, start):
+            halves = held.tile([P, 2, CHUNK], F32, name="halves")
+            nc.scalar.activation(halves[:, 0, :], bank, RELU)
+            nc.scalar.activation(halves[:, 1, :], bank, RELU, scale=-SLOPE)
+            nc.tensor.matmul(bank, identity[:], halves[:, 0, :], start=True, stop=False)
+            nc.tensor.matmul(bank, minus[:], halves[:, 1, :], start=False, stop=True)
+            largest = last.tile([P, CHUNK], F32, name="largest")
+            nc.scalar.activation(largest[:], bank, COPY)
+            nc.sync.dma_start(out[part(e), start : start + CHUNK], largest[:])
+
+        def finish_by_vector(bank, e, start):
+            sloped = last.tile([P, CHUNK], F32, name="sloped")
+            nc.scalar.activation(sloped[:], bank, COPY, scale=SLOPE)
+            largest = last.tile([P, CHUNK], F32, name="largest")
+            nc.vector.tensor_tensor(largest[:], bank, sloped[:], MAX)
+            nc.sync.dma_start(out[part(e), start : start + CHUNK], largest[:])
 
         totals = [zeros[:]] * BLOCKS
         for k in range(NEIGHBOURS):
@@ -153,4 +165,9 @@ def tile_dyngraphsage_kernel(tc, x, w, offs, out):
             totals = [pair_totals[c][:, j * CHUNK : (j + 1) * CHUNK] for c in range(BLOCKS)]
             for k in range(NEIGHBOURS // 2, NEIGHBOURS):
                 totals = add_neighbours(sums, k, start, CHUNK, totals)
-            close_straight(banks[2 + j], start, totals)
+            close_straight(banks[2 + j], totals)
+            for e in range(BLOCKS):
+                if j == 0 and e == 0:
+                    finish_by_tensor(banks[2 + j][e][:], e, start)
+                else:
+                    finish_by_vector(banks[2 + j][e][:], e, start)

@@ -12,6 +12,7 @@ NEIGHBOURS = 4
 SLOPE = 0.2
 BLOCKS = FEATURES // P
 CHUNK = 512
+HALF = CHUNK // 2
 PARTS = CHUNK // P
 PAIR = 2 * CHUNK
 PER_COLUMN = 16
@@ -49,15 +50,15 @@ def tile_dyngraphsage_kernel(tc, x, w, offs, out):
         for c in range(BLOCKS):
             nc.scalar.activation(x_bf[c][:], x_f32[c][:], COPY)
 
+        def add_neighbour(pool, c, k, start, count, total):
+            column = (k * NODES + start) // PER_COLUMN
+            picked = x_f32[c][:].indirect(offsets[:, column : column + count // PER_COLUMN])
+            longer = pool.tile([P, count], F32, name=f"sum_{count}")
+            nc.vector.tensor_tensor(longer[:], picked, total, ADD)
+            return longer[:]
+
         def add_neighbours(pool, k, start, count, totals):
-            first = (k * NODES + start) // PER_COLUMN
-            longer = []
-            for c in range(BLOCKS):
-                picked = x_f32[c][:].indirect(offsets[:, first : first + count // PER_COLUMN])
-                total = pool.tile([P, count], F32, name="total")
-                nc.vector.tensor_tensor(total[:], picked, totals[c], ADD)
-                longer.append(total[:])
-            return longer
+            return [add_neighbour(pool, c, k, start, count, totals[c]) for c in range(len(totals))]
 
         out_by_row = out.rearrange("(e p) n -> p e n", p=P)
 
@@ -119,18 +120,19 @@ def tile_dyngraphsage_kernel(tc, x, w, offs, out):
                     two = slice((b - 1) * P, (b + 1) * P)
                     nc.sync.dma_start(out_by_row[:, :, start + two.start : start + two.stop], result[:, :, two])
 
-        def close_straight(banks, totals):
+        def close_straight(banks, pieces):
             mean = moving.tile([P, BLOCKS, CHUNK], BF16, name="mean", tag=f"buffer_{PARTS - 1}")
-            for c in range(BLOCKS):
-                nc.scalar.activation(mean[:, c, :], totals[c], COPY, scale=1.0 / NEIGHBOURS)
+            for c, columns, total in pieces:
+                nc.scalar.activation(mean[:, c, columns], total, COPY, scale=1.0 / NEIGHBOURS)
                 for e in range(BLOCKS):
                     nc.tensor.matmul(
-                        banks[e][:],
+                        banks[e][:, columns],
                         w_sb[:, BLOCKS + c, part(e)],
-                        mean[:, c, :],
+                        mean[:, c, columns],
                         start=False,
-                        stop=(c == BLOCKS - 1),
+                        stop=(c == BLOCKS - 1 and columns.stop == CHUNK),
                     )
+
         def finish_by_tensor(bank, e, start):
             halves = held.tile([P, 2, CHUNK], F32, name="halves")
             nc.scalar.activation(halves[:, 0, :], bank, RELU)
@@ -163,9 +165,20 @@ def tile_dyngraphsage_kernel(tc, x, w, offs, out):
         for j in range(2):
             start = PAIR + j * CHUNK
             totals = [pair_totals[c][:, j * CHUNK : (j + 1) * CHUNK] for c in range(BLOCKS)]
+            final = totals.pop() if j == 1 else None
             for k in range(NEIGHBOURS // 2, NEIGHBOURS):
                 totals = add_neighbours(sums, k, start, CHUNK, totals)
-            close_straight(banks[2 + j], totals)
+            pieces = [(c, slice(0, CHUNK), totals[c]) for c in range(len(totals))]
+            if j == 1:
+                columns = [slice(0, HALF), slice(HALF, CHUNK)]
+                halves = [final[:, half] for half in columns]
+                for k in range(NEIGHBOURS // 2, NEIGHBOURS):
+                    halves = [
+                        add_neighbour(sums, BLOCKS - 1, k, start + columns[h].start, HALF, halves[h])
+                        for h in range(2)
+                    ]
+                pieces += [(BLOCKS - 1, columns[h], halves[h]) for h in range(2)]
+            close_straight(banks[2 + j], pieces)
             for e in range(BLOCKS):
                 if j == 0 and e == 0:
                     finish_by_tensor(banks[2 + j][e][:], e, start)

@@ -105,15 +105,15 @@ def tile_dyngraphsage_kernel(tc, x, w, offs, out):
                 terms = moving.tile([P, 2, FEATURES], F32, name="terms", tag=f"buffer_{b}")
                 nc.scalar.activation(terms[:, 0, :], v[b][:], COPY)
                 nc.scalar.activation(terms[:, 1, :], v[b][:], RELU, scale=SLOPE - 1.0)
-                for e in range(BLOCKS):
-                    for t in range(2):
+                for t in range(2):
+                    for e in range(BLOCKS):
                         nc.tensor.matmul(
                             v[b][:, part(e)],
                             terms[:, t, part(e)],
                             identity[:],
                             is_transpose=True,
-                            start=(t == 0),
-                            stop=(t == 1),
+                            start=(t == 0 and e == 0),
+                            stop=(t == 1 and e == BLOCKS - 1),
                         )
                 nc.scalar.copy(result[:, :, part(b)], v[b][:].rearrange("p (e n) -> p e n", e=BLOCKS))
                 if b % 2 == 1:

@@ -13,8 +13,10 @@ SLOPE = 0.2
 BLOCKS = FEATURES // P
 CHUNK = 512
 HALF = CHUNK // 2
-PARTS = CHUNK // P
 PAIR = 2 * CHUNK
+PARTS = PAIR // P
+BY_TENSOR = 2
+BUFFERS = 4
 PER_COLUMN = 16
 
 FLOPS = 2 * (2 * FEATURES) * FEATURES * NODES
@@ -27,9 +29,9 @@ def tile_dyngraphsage_kernel(tc, x, w, offs, out):
         tc.tile_pool(name="wide", bufs=3 * BLOCKS) as wide,
         tc.tile_pool(name="sums", bufs=3 * BLOCKS) as sums,
         tc.tile_pool(name="moving", bufs=1) as moving,
-        tc.tile_pool(name="results", bufs=2) as results,
+        tc.tile_pool(name="results", bufs=BLOCKS) as results,
         tc.tile_pool(name="last", bufs=2 * BLOCKS) as last,
-        tc.psum_pool(name="products", bufs=2 * PARTS) as products,
+        tc.psum_pool(name="products", bufs=PARTS) as products,
     ):
         offsets = held.tile([P, NEIGHBOURS * NODES // PER_COLUMN], U16, name="offsets")
         nc.sync.dma_start(offsets[:], offs)
@@ -65,12 +67,11 @@ def tile_dyngraphsage_kernel(tc, x, w, offs, out):
         def part(b):
             return slice(b * P, (b + 1) * P)
 
-        def open_turned(start):
+        def open_turned():
             v = [products.tile([P, FEATURES], F32, name="v") for b in range(PARTS)]
             for b in range(PARTS):
-                own = slice(start + b * P, start + (b + 1) * P)
                 for c in range(BLOCKS):
-                    nc.tensor.matmul(v[b][:], x_bf[c][:, own], w_sb[:, c, :], start=(c == 0), stop=False)
+                    nc.tensor.matmul(v[b][:], x_bf[c][:, part(b)], w_sb[:, c, :], start=(c == 0), stop=False)
             return v
 
         def open_straight(start):
@@ -87,7 +88,7 @@ def tile_dyngraphsage_kernel(tc, x, w, offs, out):
             return v
 
         def close_turned(v, totals):
-            mean = moving.tile([P, BLOCKS, CHUNK], BF16, name="mean", tag=f"buffer_{PARTS - 1}")
+            mean = held.tile([P, BLOCKS, PAIR], BF16, name="pair_mean")
             for c in range(BLOCKS):
                 nc.scalar.activation(mean[:, c, :], totals[c], COPY, scale=1.0 / NEIGHBOURS)
                 for b in range(PARTS):
@@ -99,29 +100,26 @@ def tile_dyngraphsage_kernel(tc, x, w, offs, out):
                         stop=(c == BLOCKS - 1),
                     )
 
-        def finish_turned(v, start):
-            result = results.tile([P, BLOCKS, CHUNK], F32, name="result")
-            for b in range(PARTS):
-                terms = moving.tile([P, 2, FEATURES], F32, name="terms", tag=f"buffer_{b}")
-                nc.scalar.activation(terms[:, 0, :], v[b][:], COPY)
-                nc.scalar.activation(terms[:, 1, :], v[b][:], RELU, scale=SLOPE - 1.0)
-                for t in range(2):
-                    for e in range(BLOCKS):
-                        nc.tensor.matmul(
-                            v[b][:, part(e)],
-                            terms[:, t, part(e)],
-                            identity[:],
-                            is_transpose=True,
-                            start=(t == 0 and e == 0),
-                            stop=(t == 1 and e == BLOCKS - 1),
-                        )
-                nc.scalar.copy(result[:, :, part(b)], v[b][:].rearrange("p (e n) -> p e n", e=BLOCKS))
-                if b % 2 == 1:
-                    two = slice((b - 1) * P, (b + 1) * P)
-                    nc.sync.dma_start(out_by_row[:, :, start + two.start : start + two.stop], result[:, :, two])
+        def finish_turned(v, b):
+            terms = moving.tile([P, 2, FEATURES], F32, name="terms", tag=f"buffer_{b % BUFFERS}")
+            nc.scalar.activation(terms[:, 0, :], v[:], COPY)
+            nc.scalar.activation(terms[:, 1, :], v[:], RELU, scale=SLOPE - 1.0)
+            for t in range(2):
+                for e in range(BLOCKS):
+                    nc.tensor.matmul(
+                        v[:, part(e)],
+                        terms[:, t, part(e)],
+                        identity[:],
+                        is_transpose=True,
+                        start=(t == 0 and e == 0),
+                        stop=(t == 1 and e == BLOCKS - 1),
+                    )
+            result = results.tile([P, BLOCKS, P], F32, name="result")
+            nc.scalar.copy(result[:], v[:].rearrange("p (e n) -> p e n", e=BLOCKS))
+            nc.sync.dma_start(out_by_row[:, :, part(b)], result[:])
 
-        def close_straight(banks, pieces):
-            mean = moving.tile([P, BLOCKS, CHUNK], BF16, name="mean", tag=f"buffer_{PARTS - 1}")
+        def close_straight(banks, pieces, tag):
+            mean = moving.tile([P, BLOCKS, CHUNK], BF16, name="mean", tag=tag)
             for c, columns, total in pieces:
                 nc.scalar.activation(mean[:, c, columns], total, COPY, scale=1.0 / NEIGHBOURS)
                 for e in range(BLOCKS):
@@ -134,7 +132,7 @@ def tile_dyngraphsage_kernel(tc, x, w, offs, out):
                     )
 
         def finish_by_tensor(bank, e, start):
-            halves = held.tile([P, 2, CHUNK], F32, name="halves")
+            halves = moving.tile([P, 2, CHUNK], F32, name="halves", tag=f"buffer_{e}")
             nc.scalar.activation(halves[:, 0, :], bank, RELU)
             nc.scalar.activation(halves[:, 1, :], bank, RELU, scale=-SLOPE)
             nc.tensor.matmul(bank, identity[:], halves[:, 0, :], start=True, stop=False)
@@ -150,37 +148,40 @@ def tile_dyngraphsage_kernel(tc, x, w, offs, out):
             nc.vector.tensor_tensor(largest[:], bank, sloped[:], MAX)
             nc.sync.dma_start(out[part(e), start : start + CHUNK], largest[:])
 
+        v = open_turned()
         totals = [zeros[:]] * BLOCKS
         for k in range(NEIGHBOURS):
             totals = add_neighbours(wide, k, 0, PAIR, totals)
-        banks = [open_turned(0), open_turned(CHUNK)]
-        for j in range(2):
-            close_turned(banks[j], [totals[c][:, j * CHUNK : (j + 1) * CHUNK] for c in range(BLOCKS)])
-            finish_turned(banks[j], j * CHUNK)
-            banks.append(open_straight(PAIR + j * CHUNK))
+        close_turned(v, totals)
+        for b in range(PARTS):
+            finish_turned(v[b], b)
 
-        pair_totals = [zeros[:]] * BLOCKS
-        for k in range(NEIGHBOURS // 2):
-            pair_totals = add_neighbours(wide, k, PAIR, PAIR, pair_totals)
-        for j in range(2):
-            start = PAIR + j * CHUNK
-            totals = [pair_totals[c][:, j * CHUNK : (j + 1) * CHUNK] for c in range(BLOCKS)]
-            final = totals.pop() if j == 1 else None
-            for k in range(NEIGHBOURS // 2, NEIGHBOURS):
-                totals = add_neighbours(sums, k, start, CHUNK, totals)
-            pieces = [(c, slice(0, CHUNK), totals[c]) for c in range(len(totals))]
-            if j == 1:
-                columns = [slice(0, HALF), slice(HALF, CHUNK)]
-                halves = [final[:, half] for half in columns]
-                for k in range(NEIGHBOURS // 2, NEIGHBOURS):
-                    halves = [
-                        add_neighbour(sums, BLOCKS - 1, k, start + columns[h].start, HALF, halves[h])
-                        for h in range(2)
-                    ]
-                pieces += [(BLOCKS - 1, columns[h], halves[h]) for h in range(2)]
-            close_straight(banks[2 + j], pieces)
-            for e in range(BLOCKS):
-                if j == 0 and e == 0:
-                    finish_by_tensor(banks[2 + j][e][:], e, start)
-                else:
-                    finish_by_vector(banks[2 + j][e][:], e, start)
+        first = add_neighbours(wide, 0, PAIR, PAIR, [zeros[:]] * BLOCKS)
+
+        third, fourth = open_straight(PAIR), open_straight(PAIR + CHUNK)
+        totals = [first[c][:, 0:CHUNK] for c in range(BLOCKS)]
+        for k in range(1, NEIGHBOURS):
+            totals = add_neighbours(sums, k, PAIR, CHUNK, totals)
+        close_straight(third, [(c, slice(0, CHUNK), totals[c]) for c in range(BLOCKS)], f"buffer_{BUFFERS - 1}")
+        for e in range(BLOCKS):
+            if e < BY_TENSOR:
+                finish_by_tensor(third[e][:], e, PAIR)
+            else:
+                finish_by_vector(third[e][:], e, PAIR)
+
+        start = PAIR + CHUNK
+        totals = add_neighbours(sums, 1, start, CHUNK, [first[c][:, CHUNK:PAIR] for c in range(BLOCKS)])
+        alone = totals.pop()
+        for k in range(2, NEIGHBOURS):
+            totals = add_neighbours(sums, k, start, CHUNK, totals)
+        pieces = [(c, slice(0, CHUNK), totals[c]) for c in range(BLOCKS - 1)]
+        columns = [slice(0, HALF), slice(HALF, CHUNK)]
+        two = [alone[:, half] for half in columns]
+        for k in range(2, NEIGHBOURS):
+            two = [
+                add_neighbour(sums, BLOCKS - 1, k, start + columns[h].start, HALF, two[h]) for h in range(2)
+            ]
+        pieces += [(BLOCKS - 1, columns[h], two[h]) for h in range(2)]
+        close_straight(fourth, pieces, f"buffer_{BY_TENSOR - 1}")
+        for e in range(BLOCKS):
+            finish_by_vector(fourth[e][:], e, start)

@@ -15,7 +15,7 @@ CHUNK = 512
 HALF = CHUNK // 2
 PAIR = 2 * CHUNK
 PARTS = PAIR // P
-BY_TENSOR = 2
+BY_TENSOR = 3
 BUFFERS = 4
 PER_COLUMN = 16
 
@@ -131,14 +131,14 @@ def tile_dyngraphsage_kernel(tc, x, w, offs, out):
                         stop=(c == BLOCKS - 1 and columns.stop == CHUNK),
                     )
 
-        def finish_by_tensor(bank, e, start):
+        def finish_by_tensor(bank, e, start, copy):
             halves = moving.tile([P, 2, CHUNK], F32, name="halves", tag=f"buffer_{e}")
             nc.scalar.activation(halves[:, 0, :], bank, RELU)
             nc.scalar.activation(halves[:, 1, :], bank, RELU, scale=-SLOPE)
             nc.tensor.matmul(bank, identity[:], halves[:, 0, :], start=True, stop=False)
             nc.tensor.matmul(bank, minus[:], halves[:, 1, :], start=False, stop=True)
             largest = last.tile([P, CHUNK], F32, name="largest")
-            nc.scalar.activation(largest[:], bank, COPY)
+            copy(largest[:], bank)
             nc.sync.dma_start(out[part(e), start : start + CHUNK], largest[:])
 
         def finish_by_vector(bank, e, start):
@@ -165,7 +165,8 @@ def tile_dyngraphsage_kernel(tc, x, w, offs, out):
         close_straight(third, [(c, slice(0, CHUNK), totals[c]) for c in range(BLOCKS)], f"buffer_{BUFFERS - 1}")
         for e in range(BLOCKS):
             if e < BY_TENSOR:
-                finish_by_tensor(third[e][:], e, PAIR)
+                copy = nc.vector.tensor_copy if e == BY_TENSOR - 1 else nc.scalar.copy
+                finish_by_tensor(third[e][:], e, PAIR, copy)
             else:
                 finish_by_vector(third[e][:], e, PAIR)
 
@@ -182,6 +183,6 @@ def tile_dyngraphsage_kernel(tc, x, w, offs, out):
                 add_neighbour(sums, BLOCKS - 1, k, start + columns[h].start, HALF, two[h]) for h in range(2)
             ]
         pieces += [(BLOCKS - 1, columns[h], two[h]) for h in range(2)]
-        close_straight(fourth, pieces, f"buffer_{BY_TENSOR - 1}")
+        close_straight(fourth, pieces, f"buffer_{BY_TENSOR - 2}")
         for e in range(BLOCKS):
             finish_by_vector(fourth[e][:], e, start)

import concourse.mybir as mybir
from concourse.masks import make_identity

F32, BF16, U16 = mybir.dt.float32, mybir.dt.bfloat16, mybir.dt.uint16
ADD, MAX = mybir.AluOpType.add, mybir.AluOpType.max
COPY, RELU = mybir.ActivationFunctionType.Copy, mybir.ActivationFunctionType.Relu

P = 128
FEATURES = 512
NODES = 2048
NEIGHBOURS = 4
SLOPE = 0.2
BLOCKS = FEATURES // P
CHUNK = 512
HALF = CHUNK // 2
PAIR = 2 * CHUNK
PARTS = PAIR // P
BY_TENSOR = 3
BUFFERS = 4
PER_COLUMN = 16

FLOPS = 2 * (2 * FEATURES) * FEATURES * NODES


def tile_dyngraphsage_kernel(tc, x, w, offs, out):
    nc = tc.nc
    with (
        tc.tile_pool(name="held", bufs=1) as held,
        tc.tile_pool(name="wide", bufs=3 * BLOCKS) as wide,
        tc.tile_pool(name="sums", bufs=3 * BLOCKS) as sums,
        tc.tile_pool(name="moving", bufs=1) as moving,
        tc.tile_pool(name="results", bufs=BLOCKS) as results,
        tc.tile_pool(name="last", bufs=2 * BLOCKS) as last,
        tc.psum_pool(name="products", bufs=PARTS) as products,
    ):
        offsets = held.tile([P, NEIGHBOURS * NODES // PER_COLUMN], U16, name="offsets")
        nc.sync.dma_start(offsets[:], offs)
        x_f32 = [held.tile([P, NODES], F32, name=f"x_f32_{c}") for c in range(BLOCKS)]
        for c in range(BLOCKS):
            nc.sync.dma_start(x_f32[c][:], x[c * P : (c + 1) * P, :])
        w_sb = held.tile([P, 2 * BLOCKS, FEATURES], BF16, name="w_sb")
        nc.sync.dma_start(w_sb[:], w.rearrange("(r p) e -> p r e", p=P))

        zeros = held.tile([P, PAIR], F32, name="zeros")
        nc.vector.memset(zeros[:], 0.0)
        identity = held.tile([P, P], F32, name="identity")
        make_identity(nc, identity[:])
        minus = held.tile([P, P], F32, name="minus")
        nc.scalar.activation(minus[:], identity[:], COPY, scale=-1.0)

        x_bf = [held.tile([P, NODES], BF16, name=f"x_bf_{c}") for c in range(BLOCKS)]
        for c in range(BLOCKS):
            nc.scalar.activation(x_bf[c][:], x_f32[c][:], COPY)

        def add_neighbour(pool, c, k, start, count, total):
            column = (k * NODES + start) // PER_COLUMN
            picked = x_f32[c][:].indirect(offsets[:, column : column + count // PER_COLUMN])
            longer = pool.tile([P, count], F32, name=f"sum_{count}")
            nc.vector.tensor_tensor(longer[:], picked, total, ADD)
            return longer[:]

        def add_neighbours(pool, k, start, count, totals):
            return [add_neighbour(pool, c, k, start, count, totals[c]) for c in range(len(totals))]

        out_by_row = out.rearrange("(e p) n -> p e n", p=P)

        def part(b):
            return slice(b * P, (b + 1) * P)

        def open_turned():
            v = [products.tile([P, FEATURES], F32, name="v") for b in range(PARTS)]
            for b in range(PARTS):
                for c in range(BLOCKS):
                    nc.tensor.matmul(v[b][:], x_bf[c][:, part(b)], w_sb[:, c, :], start=(c == 0), stop=False)
            return v

        def open_straight(start):
            v = [products.tile([P, CHUNK], F32, name="v") for e in range(BLOCKS)]
            for e in range(BLOCKS):
                for c in range(BLOCKS):
                    nc.tensor.matmul(
                        v[e][:],
                        w_sb[:, c, part(e)],
                        x_bf[c][:, start : start + CHUNK],
                        start=(c == 0),
                        stop=False,
                    )
            return v

        def close_turned(v, totals):
            mean = held.tile([P, BLOCKS, PAIR], BF16, name="pair_mean")
            for c in range(BLOCKS):
                nc.scalar.activation(mean[:, c, :], totals[c], COPY, scale=1.0 / NEIGHBOURS)
                for b in range(PARTS):
                    nc.tensor.matmul(
                        v[b][:],
                        mean[:, c, part(b)],
                        w_sb[:, BLOCKS + c, :],
                        start=False,
                        stop=(c == BLOCKS - 1),
                    )

        def finish_turned(v, b):
            terms = moving.tile([P, 2, FEATURES], F32, name="terms", tag=f"buffer_{b % BUFFERS}")
            nc.scalar.activation(terms[:, 0, :], v[:], COPY)
            nc.scalar.activation(terms[:, 1, :], v[:], RELU, scale=SLOPE - 1.0)
            for t in range(2):
                for e in range(BLOCKS):
                    nc.tensor.matmul(
                        v[:, part(e)],
                        terms[:, t, part(e)],
                        identity[:],
                        is_transpose=True,
                        start=(t == 0 and e == 0),
                        stop=(t == 1 and e == BLOCKS - 1),
                    )
            result = results.tile([P, BLOCKS, P], F32, name="result")
            nc.scalar.copy(result[:], v[:].rearrange("p (e n) -> p e n", e=BLOCKS))
            nc.sync.dma_start(out_by_row[:, :, part(b)], result[:])

        def close_straight(banks, pieces, tag):
            mean = moving.tile([P, BLOCKS, CHUNK], BF16, name="mean", tag=tag)
            for c, columns, total in pieces:
                nc.scalar.activation(mean[:, c, columns], total, COPY, scale=1.0 / NEIGHBOURS)
                for e in range(BLOCKS):
                    nc.tensor.matmul(
                        banks[e][:, columns],
                        w_sb[:, BLOCKS + c, part(e)],
                        mean[:, c, columns],
                        start=False,
                        stop=(c == BLOCKS - 1 and columns.stop == CHUNK),
                    )

        def finish_by_tensor(bank, e, start, copy):
            halves = moving.tile([P, 2, CHUNK], F32, name="halves", tag=f"buffer_{e}")
            nc.scalar.activation(halves[:, 0, :], bank, RELU)
            nc.scalar.activation(halves[:, 1, :], bank, RELU, scale=-SLOPE)
            nc.tensor.matmul(bank, identity[:], halves[:, 0, :], start=True, stop=False)
            nc.tensor.matmul(bank, minus[:], halves[:, 1, :], start=False, stop=True)
            largest = last.tile([P, CHUNK], F32, name="largest")
            copy(largest[:], bank)
            nc.sync.dma_start(out[part(e), start : start + CHUNK], largest[:])

        def finish_by_vector(bank, e, start):
            sloped = last.tile([P, CHUNK], F32, name="sloped")
            nc.scalar.activation(sloped[:], bank, COPY, scale=SLOPE)
            largest = last.tile([P, CHUNK], F32, name="largest")
            nc.vector.tensor_tensor(largest[:], bank, sloped[:], MAX)
            nc.sync.dma_start(out[part(e), start : start + CHUNK], largest[:])

        v = open_turned()
        totals = [zeros[:]] * BLOCKS
        for k in range(NEIGHBOURS):
            totals = add_neighbours(wide, k, 0, PAIR, totals)
        close_turned(v, totals)
        for b in range(PARTS):
            finish_turned(v[b], b)

        first = add_neighbours(wide, 0, PAIR, PAIR, [zeros[:]] * BLOCKS)

        third, fourth = open_straight(PAIR), open_straight(PAIR + CHUNK)
        totals = [first[c][:, 0:CHUNK] for c in range(BLOCKS)]
        for k in range(1, NEIGHBOURS):
            totals = add_neighbours(sums, k, PAIR, CHUNK, totals)
        close_straight(third, [(c, slice(0, CHUNK), totals[c]) for c in range(BLOCKS)], f"buffer_{BUFFERS - 1}")
        for e in range(BLOCKS):
            if e < BY_TENSOR:
                copy = nc.vector.tensor_copy if e == BY_TENSOR - 1 else nc.scalar.copy
                finish_by_tensor(third[e][:], e, PAIR, copy)
            else:
                finish_by_vector(third[e][:], e, PAIR)

        start = PAIR + CHUNK
        totals = add_neighbours(sums, 1, start, CHUNK, [first[c][:, CHUNK:PAIR] for c in range(BLOCKS)])
        alone = totals.pop()
        for k in range(2, NEIGHBOURS):
            totals = add_neighbours(sums, k, start, CHUNK, totals)
        pieces = [(c, slice(0, CHUNK), totals[c]) for c in range(BLOCKS - 1)]
        columns = [slice(0, HALF), slice(HALF, CHUNK)]
        two = [alone[:, half] for half in columns]
        for k in range(2, NEIGHBOURS):
            two = [
                add_neighbour(sums, BLOCKS - 1, k, start + columns[h].start, HALF, two[h]) for h in range(2)
            ]
        pieces += [(BLOCKS - 1, columns[h], two[h]) for h in range(2)]
        close_straight(fourth, pieces, f"buffer_{BY_TENSOR - 2}")
        for e in range(BLOCKS):
            finish_by_vector(fourth[e][:], e, start)
